import numpy as np
import ml_dtypes


def mxq(x, axis, fmt="e4m3"):
    dtype, down = {"e4m3": (ml_dtypes.float8_e4m3fn, 7), "e5m2": (ml_dtypes.float8_e5m2, 14)}[fmt]
    v = np.moveaxis(np.asarray(x, np.float32).astype(ml_dtypes.bfloat16).astype(np.float64), axis, -1)
    blocks = v.reshape(v.shape[:-1] + (-1, 32))
    amax = np.abs(blocks).max(-1, keepdims=True)
    byte = np.maximum(np.where(amax > 0, np.frexp(amax)[1] - 1 + 127, 0) - down, 1)
    scale = np.exp2(byte - 127.0)
    codes = (blocks / scale).astype(np.float32).astype(dtype).astype(np.float64)
    return np.moveaxis((codes * scale).reshape(v.shape), -1, axis)


WIDE = False


def mx_kscale(k):
    if not WIDE:
        return np.ones(k)
    levels = np.array([10, -10, 5, -5, 0])
    a = np.random.permutation(np.resize(levels, k // 512 * 4)).reshape(k // 512, 4)
    idx = np.arange(k)
    return np.exp2(a[idx // 512, idx % 128 // 32])


BF16 = ml_dtypes.bfloat16


def bf(x):
    return np.asarray(x, np.float32).astype(BF16)


def f64(x):
    return np.asarray(x).astype(np.float64)


B, IN, HID, OUT, LAYERS, NG = 4096, 512, 512, 256, 2, 4
GW = NG * HID
LN_EPS = 1e-5
SIG_MIN = 1e-6


def sigmoid(v):
    return 1.0 / (1.0 + np.exp(-v))


def softplus(v):
    return np.log(1.0 + np.exp(v))


def setup_inputs():
    s = mx_kscale(HID)
    return {
        "h1": bf(np.random.standard_normal((B, HID)) * 0.3 * s),
        "W_ih1": bf(np.random.standard_normal((GW, HID)) * 3.0 / np.sqrt(HID) / s),
        "hh_gates": bf(np.random.standard_normal(GW) * 0.5),
        "b_ih1": bf(np.random.standard_normal(GW) * 0.3),
        "b_hh1": bf(np.random.standard_normal(GW) * 0.3),
        "c_init": bf(np.random.standard_normal(HID)),
        "mu_W": bf(np.random.standard_normal((OUT, HID)) * 3.0 / np.sqrt(HID)),
        "mu_b": bf(np.random.standard_normal(OUT) * 0.3 + 0.3),
        "ln_g": bf(1.0 + 0.1 * np.random.standard_normal(OUT)),
        "ln_b": bf(0.1 * np.random.standard_normal(OUT)),
        "sig_W": bf(np.random.standard_normal((OUT, HID)) * 3.0 / np.sqrt(HID)),
        "sig_b": bf(np.random.standard_normal(OUT) * 0.3),
    }


def reference(h1, W_ih1, hh_gates, b_ih1, b_hh1, c_init, mu_W, mu_b, ln_g, ln_b, sig_W, sig_b):
    gates = (mxq(f64(h1), 1, "e4m3") @ mxq(f64(W_ih1).T, 0, "e4m3")) + f64(hh_gates) + (f64(b_ih1) + f64(b_hh1))
    i, f, g, o = np.split(gates, NG, axis=-1)
    i, f, o = sigmoid(i), sigmoid(f), sigmoid(o)
    g = np.tanh(g)
    c_new = f * f64(c_init) + i * g
    h2 = o * np.tanh(c_new)
    hq = mxq(h2, 1, "e4m3")
    mu_lin = (hq @ mxq(f64(mu_W).T, 0, "e4m3")) + f64(mu_b)
    mean = mu_lin.mean(axis=-1, keepdims=True)
    var = np.square(mu_lin - mean).mean(axis=-1, keepdims=True)
    mu = (mu_lin - mean) * (1.0 / np.sqrt(var + LN_EPS)) * f64(ln_g) + f64(ln_b)
    sigma = softplus((hq @ mxq(f64(sig_W).T, 0, "e4m3")) + f64(sig_b)) + SIG_MIN
    return mu, sigma

@@ -1,0 +1,250 @@
+from contextlib import ExitStack
+
+import concourse.mybir as mybir
+from concourse.masks import make_identity
+
+F32 = mybir.dt.float32
+BF16 = mybir.dt.bfloat16
+U32 = mybir.dt.uint32
+U8 = mybir.dt.uint8
+FP8X4 = mybir.dt.float8_e4m3fn_x4
+ACT = mybir.ActivationFunctionType
+ALU = mybir.AluOpType
+
+P = 128
+PACK = 4
+K = P * PACK
+
+BATCH, HID, OUT, NG = 4096, 512, 256, 4
+ROWS = 512
+NBLK = BATCH // ROWS
+GATE_I, GATE_F, GATE_G, GATE_O = 0, 1, 2, 3
+GATE_ORDER = (GATE_I, GATE_G, GATE_F, GATE_O)
+LN_EPS = 1e-5
+SIG_MIN = 1e-6
+SOFTPLUS_LINEAR_FROM = 32.0
+NORM_LAG = 2
+
+FLOPS = 2 * BATCH * HID * (NG * HID) + 2 * BATCH * HID * (2 * OUT)
+
+
+def quantise_512_rows(nc, psum, stage, identity, raw, codes, scales):
+    words = raw.bitcast(F32).rearrange("r (a q u) -> r a u q", a=PACK, u=2)
+    grouped = stage.tile([P, ROWS * PACK], BF16, align_bytes=64)
+    grouped_words = grouped[:].bitcast(F32).rearrange("q (a r u) -> q a r u", a=PACK, u=2)
+    for half in range(2):
+        bank = psum.tile([P, 2, 2, P], F32, tag="transposed")
+        for a in range(2):
+            for u in range(2):
+                nc.tensor.transpose(bank[:, a, u, :], words[:, 2 * half + a, u, :], identity)
+        copy = nc.scalar.copy if half == 0 else nc.vector.tensor_copy
+        copy(
+            out=grouped_words[:, 2 * half : 2 * half + 2, :, :],
+            in_=bank[:].rearrange("q a u r -> q a r u"),
+        )
+    nc.vector.quantize_mx(out=codes.bitcast(FP8X4), scales=scales, in_=grouped[:])
+
+
+def tile_rdecommunicationlstm_pb_t_kernel(
+    tc, h1, W_ih1, hh_gates, b_ih1, b_hh1, c_init, mu_W, mu_b, ln_g, ln_b, sig_W, sig_b, out_0, out_1
+):
+    nc = tc.nc
+    with ExitStack() as whole_kernel:
+        consts = whole_kernel.enter_context(tc.tile_pool(name="consts", bufs=1))
+        norm = whole_kernel.enter_context(tc.tile_pool(name="norm", bufs=2))
+        psum_t = whole_kernel.enter_context(tc.psum_pool(name="psum_t", bufs=2))
+        psum_gate = whole_kernel.enter_context(tc.psum_pool(name="psum_gate", bufs=4))
+        psum_head = whole_kernel.enter_context(tc.psum_pool(name="psum_head", bufs=2))
+
+        warm = consts.tile([P, 1], F32)
+        nc.vector.memset(warm[:], 0.0)
+        nc.scalar.activation(out=warm[:], in_=warm[:], func=ACT.Sigmoid)
+
+        identity = consts.tile([P, P], F32)
+        make_identity(nc, identity[:])
+
+        lin = consts.tile([P, NBLK, 2, PACK, OUT], F32)
+        mean_var = consts.tile([P, NBLK, PACK, 2], F32)
+        var_eps = consts.tile([P, NBLK, PACK], F32)
+        rstd = consts.tile([P, NBLK, PACK], F32)
+        minus_half = consts.tile([P, PACK], F32)
+        nc.vector.memset(minus_half[:], -0.5)
+
+        def normalise(n):
+            for j in range(PACK):
+                centred = norm.tile([P, OUT], F32)
+                nc.vector.scalar_tensor_tensor(
+                    out=centred[:], in0=lin[:, n, 0, j, :], scalar=mean_var[:, n, j, 0:1], in1=ln_g_all,
+                    op0=ALU.subtract, op1=ALU.mult,
+                )
+                nc.vector.scalar_tensor_tensor(
+                    out=lin[:, n, 0, j, :], in0=centred[:], scalar=rstd[:, n, j : j + 1], in1=ln_b_all,
+                    op0=ALU.mult, op1=ALU.add,
+                )
+            nc.sync.dma_start(
+                out=out_0[n * ROWS : (n + 1) * ROWS, :].rearrange("(r j) c -> r j c", j=PACK),
+                in_=lin[:, n, 0, :, :],
+            )
+
+        with ExitStack() as main_loop:
+            weights = main_loop.enter_context(tc.tile_pool(name="weights", bufs=1))
+            h1_raw_pool = main_loop.enter_context(tc.tile_pool(name="h1_raw", bufs=4))
+            stage = main_loop.enter_context(tc.tile_pool(name="stage", bufs=2))
+            gates = main_loop.enter_context(tc.tile_pool(name="gates", bufs=2))
+
+            def load_h1(n):
+                h1_raw = h1_raw_pool.tile([P, PACK * K], BF16)
+                nc.sync.dma_start(
+                    out=h1_raw[:],
+                    in_=h1[n * ROWS : (n + 1) * ROWS, :].rearrange("(r j) k -> r (j k)", j=PACK),
+                )
+                return h1_raw
+
+            h1_raw = {0: load_h1(0)}
+            w_raw = {}
+            for g in GATE_ORDER:
+                w_raw[g] = weights.tile([P, PACK * K], BF16, name="w_raw%d" % g)
+                nc.sync.dma_start(
+                    out=w_raw[g][:],
+                    in_=W_ih1[g * HID : (g + 1) * HID, :].rearrange("(m t) k -> m (t k)", t=PACK),
+                )
+            head_raw = weights.tile([P, PACK * K], BF16)
+            head_raw_tiles = head_raw[:].rearrange("r (a k) -> r a k", a=PACK)
+            nc.sync.dma_start(out=head_raw_tiles[:, 0:2, :], in_=mu_W.rearrange("(a r) k -> r a k", a=2))
+            nc.sync.dma_start(out=head_raw_tiles[:, 2:4, :], in_=sig_W.rearrange("(a r) k -> r a k", a=2))
+
+            bias_parts = []
+            for vector in (hh_gates, b_ih1, b_hh1):
+                part = consts.tile([P, NG, PACK], BF16, name="bias_part%d" % len(bias_parts))
+                nc.scalar.dma_start(out=part[:], in_=vector.rearrange("(g m t) -> m g t", g=NG, t=PACK))
+                bias_parts.append(part)
+            c_init_bf = consts.tile([P, PACK], BF16)
+            nc.scalar.dma_start(out=c_init_bf[:], in_=c_init.rearrange("(m t) -> m t", t=PACK))
+            gate_bias = consts.tile([P, NG, PACK], F32)
+            nc.vector.tensor_tensor(out=gate_bias[:], in0=bias_parts[1][:], in1=bias_parts[2][:], op=ALU.add)
+            nc.vector.tensor_tensor(out=gate_bias[:], in0=gate_bias[:], in1=bias_parts[0][:], op=ALU.add)
+            c_init_f = consts.tile([P, PACK], F32)
+            nc.vector.tensor_copy(out=c_init_f[:], in_=c_init_bf[:])
+
+            head_rows = weights.tile([P, 4 * OUT], BF16)
+            nc.vector.memset(head_rows[:], 0.0)
+            for slot, vector in enumerate((mu_b, sig_b, ln_g, ln_b)):
+                nc.scalar.dma_start(out=head_rows[0:1, slot * OUT : (slot + 1) * OUT], in_=vector.unsqueeze(0))
+            ones = weights.tile([P, P], BF16)
+            nc.vector.memset(ones[:], 1.0)
+            spread = consts.tile([P, 4 * OUT], F32)
+            for half in range(2):
+                cols = slice(half * 2 * OUT, (half + 1) * 2 * OUT)
+                spread_ps = psum_head.tile([P, 2 * OUT], F32, tag="head")
+                nc.tensor.matmul(out=spread_ps[:], lhsT=ones[:], rhs=head_rows[:, cols], start=True, stop=True)
+                nc.vector.tensor_copy(out=spread[:, cols], in_=spread_ps[:])
+            head_bias = spread[:, 0 : 2 * OUT].rearrange("r (h c) -> r h c", h=2)
+            ln_g_all = spread[:, 2 * OUT : 3 * OUT]
+            ln_b_all = spread[:, 3 * OUT : 4 * OUT]
+
+            def quantise_h1(n):
+                codes = stage.tile([P, ROWS], U32, name="h1_codes", align_bytes=64)
+                scales = stage.tile([P, ROWS], U8, name="h1_scales", align_bytes=64)
+                quantise_512_rows(nc, psum_t, stage, identity[:], h1_raw[n][:], codes[:], scales[:])
+                return codes, scales
+
+            h1_q = {0: quantise_h1(0)}
+            w_codes, w_scales = {}, {}
+            for g in GATE_ORDER:
+                w_codes[g] = weights.tile([P, ROWS], U32, name="w_codes%d" % g, align_bytes=64)
+                w_scales[g] = weights.tile([P, ROWS], U8, name="w_scales%d" % g, align_bytes=64)
+                quantise_512_rows(nc, psum_t, stage, identity[:], w_raw[g][:], w_codes[g][:], w_scales[g][:])
+            head_codes = weights.tile([P, ROWS], U32, align_bytes=64)
+            head_scales = weights.tile([P, ROWS], U8, align_bytes=64)
+            quantise_512_rows(nc, psum_t, stage, identity[:], head_raw[:], head_codes[:], head_scales[:])
+            for n in range(1, 4):
+                h1_raw[n] = load_h1(n)
+
+            for n in range(NBLK):
+                if n + 4 < NBLK:
+                    h1_raw[n + 4] = load_h1(n + 4)
+                if n + 1 < NBLK:
+                    h1_q[n + 1] = quantise_h1(n + 1)
+                codes, scales = h1_q[n]
+
+                act = {}
+                for g in GATE_ORDER:
+                    act[g] = gates.tile([P, PACK, ROWS], F32, name="gate%d" % g)
+                    for t in range(PACK):
+                        units = slice(t * P, (t + 1) * P)
+                        gate_ps = psum_gate.tile([P, ROWS], F32, tag="gate")
+                        nc.tensor.matmul_mx(
+                            out=gate_ps[:],
+                            lhsT=w_codes[g][:, units].bitcast(FP8X4), lhsT_scale=w_scales[g][:, units],
+                            rhs=codes[:].bitcast(FP8X4), rhs_scale=scales[:],
+                            start=True, stop=True,
+                        )
+                        nc.scalar.activation(
+                            out=act[g][:, t, :], in_=gate_ps[:],
+                            func=ACT.Tanh if g == GATE_G else ACT.Sigmoid,
+                            bias=gate_bias[:, g, t : t + 1], scale=1.0,
+                        )
+                    if g == GATE_G:
+                        nc.vector.tensor_tensor(out=act[GATE_I][:], in0=act[GATE_I][:], in1=act[GATE_G][:], op=ALU.mult)
+                    if g == GATE_F:
+                        for t in range(PACK):
+                            nc.vector.scalar_tensor_tensor(
+                                out=act[GATE_F][:, t, :], in0=act[GATE_F][:, t, :], scalar=c_init_f[:, t : t + 1],
+                                in1=act[GATE_I][:, t, :], op0=ALU.mult, op1=ALU.add,
+                            )
+                cell = act[GATE_F]
+                nc.scalar.activation(out=cell[:], in_=cell[:], func=ACT.Tanh)
+
+                h2 = stage.tile([P, ROWS * PACK], BF16, align_bytes=64)
+                nc.vector.tensor_tensor(
+                    out=h2[:].rearrange("m (c i t) -> m c t i", i=4, t=PACK),
+                    in0=act[GATE_O][:].rearrange("m t (c i) -> m c t i", i=4),
+                    in1=cell[:].rearrange("m t (c i) -> m c t i", i=4),
+                    op=ALU.mult,
+                )
+                h2_codes = stage.tile([P, ROWS], U32, align_bytes=64)
+                h2_scales = stage.tile([P, ROWS], U8, align_bytes=64)
+                nc.vector.quantize_mx(out=h2_codes[:].bitcast(FP8X4), scales=h2_scales[:], in_=h2[:])
+
+                stats = norm.tile([P, PACK, 6], F32)
+                for j in range(PACK):
+                    rows = slice(j * P, (j + 1) * P)
+                    head_ps = psum_head.tile([P, 2 * OUT], F32, tag="head")
+                    nc.tensor.matmul_mx(
+                        out=head_ps[:],
+                        lhsT=h2_codes[:, rows].bitcast(FP8X4), lhsT_scale=h2_scales[:, rows],
+                        rhs=head_codes[:].bitcast(FP8X4), rhs_scale=head_scales[:],
+                        start=True, stop=True,
+                    )
+                    nc.vector.tensor_tensor(
+                        out=lin[:, n, :, j, :], in0=head_ps[:].rearrange("r (h c) -> r h c", h=2), in1=head_bias,
+                        op=ALU.add,
+                    )
+                    nc.vector.bn_stats(out=stats[:, j, :], in_=lin[:, n, 0, j, :])
+                    nc.vector.bn_aggr(out=mean_var[:, n, j, :], in_=stats[:, j, :])
+                nc.vector.tensor_scalar_add(out=var_eps[:, n, :], in0=mean_var[:, n, :, 1], scalar1=LN_EPS)
+                nc.gpsimd.tensor_tensor(out=rstd[:, n, :], in0=var_eps[:, n, :], in1=minus_half[:], op=ALU.pow)
+                if n >= NORM_LAG:
+                    normalise(n - NORM_LAG)
+
+        with tc.tile_pool(name="softplus", bufs=NBLK) as softplus:
+            exps = []
+            for n in range(NBLK):
+                v = lin[:, n, 1, :, :].rearrange("r j c -> r (j c)")
+                e = softplus.tile([P, PACK * OUT], F32)
+                nc.vector.tensor_scalar_min(out=e[:], in0=v, scalar1=SOFTPLUS_LINEAR_FROM)
+                nc.scalar.activation(out=e[:], in_=e[:], func=ACT.Exp)
+                exps.append(e)
+            for n in range(NBLK - NORM_LAG, NBLK):
+                normalise(n)
+            for n in range(NBLK):
+                v = lin[:, n, 1, :, :].rearrange("r j c -> r (j c)")
+                e = exps[n]
+                nc.scalar.activation(out=e[:], in_=e[:], func=ACT.Ln, bias=1.0, scale=1.0)
+                nc.vector.scalar_tensor_tensor(
+                    out=v, in0=e[:], scalar=SIG_MIN, in1=v, op0=ALU.add, op1=ALU.max,
+                )
+                nc.sync.dma_start(
+                    out=out_1[n * ROWS : (n + 1) * ROWS, :].rearrange("(r j) c -> r j c", j=PACK),
+                    in_=lin[:, n, 1, :, :],
+                )

@@ -184,8 +184,10 @@ def tile_rdecommunicationlstm_pb_t_kernel(
                             func=ACT.Tanh if g == GATE_G else ACT.Sigmoid,
                             bias=gate_bias[:, g, t : t + 1], scale=1.0,
                         )
-                    if g == GATE_G:
-                        nc.vector.tensor_tensor(out=act[GATE_I][:], in0=act[GATE_I][:], in1=act[GATE_G][:], op=ALU.mult)
+                        if g == GATE_G:
+                            nc.gpsimd.tensor_tensor(
+                                out=act[GATE_I][:, t, :], in0=act[GATE_I][:, t, :], in1=act[GATE_G][:, t, :], op=ALU.mult
+                            )
                     if g == GATE_F:
                         for t in range(PACK):
                             nc.vector.scalar_tensor_tensor(

@@ -23,12 +23,13 @@ GATE_ORDER = (GATE_I, GATE_G, GATE_F, GATE_O)
 LN_EPS = 1e-5
 SIG_MIN = 1e-6
 SOFTPLUS_LINEAR_FROM = 32.0
-NORM_LAG = 2
+
+FILL_BLOCKS = 1
 
 FLOPS = 2 * BATCH * HID * (NG * HID) + 2 * BATCH * HID * (2 * OUT)
 
 
-def quantise_512_rows(nc, psum, stage, identity, raw, codes, scales):
+def regroup_512_rows(nc, psum, stage, identity, raw, copy_out):
     words = raw.bitcast(F32).rearrange("r (a q u) -> r a u q", a=PACK, u=2)
     grouped = stage.tile([P, ROWS * PACK], BF16, align_bytes=64)
     grouped_words = grouped[:].bitcast(F32).rearrange("q (a r u) -> q a r u", a=PACK, u=2)
@@ -37,42 +38,167 @@ def quantise_512_rows(nc, psum, stage, identity, raw, codes, scales):
         for a in range(2):
             for u in range(2):
                 nc.tensor.transpose(bank[:, a, u, :], words[:, 2 * half + a, u, :], identity)
-        copy = nc.scalar.copy if half == 0 else nc.vector.tensor_copy
-        copy(
+        copy_out(
             out=grouped_words[:, 2 * half : 2 * half + 2, :, :],
             in_=bank[:].rearrange("q a u r -> q a r u"),
         )
-    nc.vector.quantize_mx(out=codes.bitcast(FP8X4), scales=scales, in_=grouped[:])
+    return grouped
 
 
 def tile_rdecommunicationlstm_pb_t_kernel(
     tc, h1, W_ih1, hh_gates, b_ih1, b_hh1, c_init, mu_W, mu_b, ln_g, ln_b, sig_W, sig_b, out_0, out_1
 ):
     nc = tc.nc
-    with ExitStack() as whole_kernel:
-        consts = whole_kernel.enter_context(tc.tile_pool(name="consts", bufs=1))
-        norm = whole_kernel.enter_context(tc.tile_pool(name="norm", bufs=2))
-        psum_t = whole_kernel.enter_context(tc.psum_pool(name="psum_t", bufs=2))
-        psum_gate = whole_kernel.enter_context(tc.psum_pool(name="psum_gate", bufs=4))
-        psum_head = whole_kernel.enter_context(tc.psum_pool(name="psum_head", bufs=2))
+    with ExitStack() as pools:
+        consts = pools.enter_context(tc.tile_pool(name="consts", bufs=1))
+        raw_pool = pools.enter_context(tc.tile_pool(name="raw", bufs=5))
+        stage = pools.enter_context(tc.tile_pool(name="stage", bufs=2))
+        softplus = pools.enter_context(tc.tile_pool(name="softplus", bufs=NBLK))
+        psum_t = pools.enter_context(tc.psum_pool(name="psum_t", bufs=2))
+        psum_gate = pools.enter_context(tc.psum_pool(name="psum_gate", bufs=4))
+        psum_head = pools.enter_context(tc.psum_pool(name="psum_head", bufs=2))
+
+        def load_rows(source):
+            raw = raw_pool.tile([P, PACK * K], BF16, name="raw")
+            nc.sync.dma_start(out=raw[:], in_=source)
+            return raw
+
+        def h1_rows(n):
+            return h1[n * ROWS : (n + 1) * ROWS, :].rearrange("(r j) k -> r (j k)", j=PACK)
+
+        bias_parts = []
+        for vector in (hh_gates, b_ih1, b_hh1):
+            part = consts.tile([P, NG, PACK], BF16, name="bias_part%d" % len(bias_parts))
+            nc.scalar.dma_start(out=part[:], in_=vector.rearrange("(g m t) -> m g t", g=NG, t=PACK))
+            bias_parts.append(part)
+        c_init_bf = consts.tile([P, PACK], BF16)
+        nc.scalar.dma_start(out=c_init_bf[:], in_=c_init.rearrange("(m t) -> m t", t=PACK))
+
+        h1_raw = {0: load_rows(h1_rows(0))}
+        w_raw = {}
+        for g in GATE_ORDER:
+            w_raw[g] = load_rows(W_ih1[g * HID : (g + 1) * HID, :].rearrange("(m t) k -> m (t k)", t=PACK))
+        h1_raw[1] = load_rows(h1_rows(1))
+        head_raw = raw_pool.tile([P, PACK * K], BF16, name="raw")
+        head_raw_tiles = head_raw[:].rearrange("r (a k) -> r a k", a=PACK)
+        nc.sync.dma_start(out=head_raw_tiles[:, 0:2, :], in_=mu_W.rearrange("(a r) k -> r a k", a=2))
+        nc.sync.dma_start(out=head_raw_tiles[:, 2:4, :], in_=sig_W.rearrange("(a r) k -> r a k", a=2))
+        head_rows = consts.tile([P, 4 * OUT], BF16)
+        nc.vector.memset(head_rows[:], 0.0)
+        for slot, vector in enumerate((mu_b, sig_b, ln_g, ln_b)):
+            nc.sync.dma_start(out=head_rows[0:1, slot * OUT : (slot + 1) * OUT], in_=vector.unsqueeze(0))
+        for n in range(2, NBLK):
+            h1_raw[n] = load_rows(h1_rows(n))
 
         warm = consts.tile([P, 1], F32)
         nc.vector.memset(warm[:], 0.0)
         nc.scalar.activation(out=warm[:], in_=warm[:], func=ACT.Sigmoid)
-
         identity = consts.tile([P, P], F32)
         make_identity(nc, identity[:])
+        ones = consts.tile([P, P], BF16)
+        nc.vector.memset(ones[:], 1.0)
+        minus_half = consts.tile([P, PACK], F32)
+        nc.vector.memset(minus_half[:], -0.5)
+        gate_bias = consts.tile([P, NG, PACK], F32)
+        nc.vector.tensor_tensor(out=gate_bias[:], in0=bias_parts[1][:], in1=bias_parts[2][:], op=ALU.add)
+        nc.vector.tensor_tensor(out=gate_bias[:], in0=gate_bias[:], in1=bias_parts[0][:], op=ALU.add)
+        c_init_f = consts.tile([P, PACK], F32)
+        nc.vector.tensor_copy(out=c_init_f[:], in_=c_init_bf[:])
 
         lin = consts.tile([P, NBLK, 2, PACK, OUT], F32)
         mean_var = consts.tile([P, NBLK, PACK, 2], F32)
         var_eps = consts.tile([P, NBLK, PACK], F32)
         rstd = consts.tile([P, NBLK, PACK], F32)
-        minus_half = consts.tile([P, PACK], F32)
-        nc.vector.memset(minus_half[:], -0.5)
 
-        def normalise(n):
+        h1_grouped, h1_q, act, h2, h2_q, exps = {}, {}, {}, {}, {}, {}
+
+        def regroup_h1(n):
+            copy_out = nc.vector.tensor_copy if n < FILL_BLOCKS else nc.scalar.copy
+            h1_grouped[n] = regroup_512_rows(nc, psum_t, stage, identity[:], h1_raw[n][:], copy_out)
+
+        def quantise_h1(n):
+            codes = stage.tile([P, ROWS], U32, name="h1_codes", align_bytes=64)
+            scales = stage.tile([P, ROWS], U8, name="h1_scales", align_bytes=64)
+            nc.vector.quantize_mx(out=codes[:].bitcast(FP8X4), scales=scales[:], in_=h1_grouped[n][:])
+            h1_q[n] = (codes, scales)
+
+        def gate(n, g):
+            codes, scales = h1_q[n]
+            act[n, g] = gates.tile([P, PACK, ROWS], F32, name="gate%d" % g)
+            for t in range(PACK):
+                units = slice(t * P, (t + 1) * P)
+                gate_ps = psum_gate.tile([P, ROWS], F32, tag="gate")
+                nc.tensor.matmul_mx(
+                    out=gate_ps[:],
+                    lhsT=w_codes[g][:, units].bitcast(FP8X4), lhsT_scale=w_scales[g][:, units],
+                    rhs=codes[:].bitcast(FP8X4), rhs_scale=scales[:],
+                    start=True, stop=True,
+                )
+                nc.scalar.activation(
+                    out=act[n, g][:, t, :], in_=gate_ps[:],
+                    func=ACT.Tanh if g == GATE_G else ACT.Sigmoid,
+                    bias=gate_bias[:, g, t : t + 1], scale=1.0,
+                )
+
+        def input_times_candidate(n):
+            nc.vector.tensor_tensor(out=act[n, GATE_I][:], in0=act[n, GATE_I][:], in1=act[n, GATE_G][:], op=ALU.mult)
+
+        def new_cell(n):
+            for t in range(PACK):
+                nc.vector.scalar_tensor_tensor(
+                    out=act[n, GATE_F][:, t, :], in0=act[n, GATE_F][:, t, :], scalar=c_init_f[:, t : t + 1],
+                    in1=act[n, GATE_I][:, t, :], op0=ALU.mult, op1=ALU.add,
+                )
+
+        def tanh_cell(n):
+            for t in range(PACK):
+                nc.scalar.activation(out=act[n, GATE_F][:, t, :], in_=act[n, GATE_F][:, t, :], func=ACT.Tanh)
+
+        def hidden(n):
+            h2[n] = stage.tile([P, ROWS * PACK], BF16, name="h2", align_bytes=64)
+            nc.vector.tensor_tensor(
+                out=h2[n][:].rearrange("m (c i t) -> m c t i", i=4, t=PACK),
+                in0=act[n, GATE_O][:].rearrange("m t (c i) -> m c t i", i=4),
+                in1=act[n, GATE_F][:].rearrange("m t (c i) -> m c t i", i=4),
+                op=ALU.mult,
+            )
+
+        def quantise_hidden(n):
+            codes = stage.tile([P, ROWS], U32, name="h2_codes", align_bytes=64)
+            scales = stage.tile([P, ROWS], U8, name="h2_scales", align_bytes=64)
+            nc.vector.quantize_mx(out=codes[:].bitcast(FP8X4), scales=scales[:], in_=h2[n][:])
+            h2_q[n] = (codes, scales)
+
+        def heads(n):
+            codes, scales = h2_q[n]
+            stats = stage.tile([P, PACK, 6], F32, name="stats")
             for j in range(PACK):
-                centred = norm.tile([P, OUT], F32)
+                rows = slice(j * P, (j + 1) * P)
+                head_ps = psum_head.tile([P, 2 * OUT], F32, tag="head")
+                nc.tensor.matmul_mx(
+                    out=head_ps[:],
+                    lhsT=codes[:, rows].bitcast(FP8X4), lhsT_scale=scales[:, rows],
+                    rhs=head_codes[:].bitcast(FP8X4), rhs_scale=head_scales[:],
+                    start=True, stop=True,
+                )
+                nc.vector.tensor_tensor(
+                    out=lin[:, n, :, j, :], in0=head_ps[:].rearrange("r (h c) -> r h c", h=2), in1=head_bias,
+                    op=ALU.add,
+                )
+                nc.vector.bn_stats(out=stats[:, j, :], in_=lin[:, n, 0, j, :])
+                nc.vector.bn_aggr(out=mean_var[:, n, j, :], in_=stats[:, j, :])
+            nc.vector.tensor_scalar_add(out=var_eps[:, n, :], in0=mean_var[:, n, :, 1], scalar1=LN_EPS)
+            nc.gpsimd.tensor_tensor(out=rstd[:, n, :], in0=var_eps[:, n, :], in1=minus_half[:], op=ALU.pow)
+
+        def clamp(n):
+            exps[n] = softplus.tile([P, PACK * OUT], F32, name="exps")
+            nc.vector.tensor_scalar_min(
+                out=exps[n][:], in0=lin[:, n, 1, :, :].rearrange("r j c -> r (j c)"), scalar1=SOFTPLUS_LINEAR_FROM
+            )
+
+        def normalise(n, tiles):
+            for j in tiles:
+                centred = stage.tile([P, OUT], F32, name="centred")
                 nc.vector.scalar_tensor_tensor(
                     out=centred[:], in0=lin[:, n, 0, j, :], scalar=mean_var[:, n, j, 0:1], in1=ln_g_all,
                     op0=ALU.subtract, op1=ALU.mult,
@@ -81,170 +207,92 @@ def tile_rdecommunicationlstm_pb_t_kernel(
                     out=lin[:, n, 0, j, :], in0=centred[:], scalar=rstd[:, n, j : j + 1], in1=ln_b_all,
                     op0=ALU.mult, op1=ALU.add,
                 )
+
+        def normalise_first_half(n):
+            normalise(n, (0, 1))
+
+        def normalise_second_half(n):
+            normalise(n, (2, 3))
             nc.sync.dma_start(
                 out=out_0[n * ROWS : (n + 1) * ROWS, :].rearrange("(r j) c -> r j c", j=PACK),
                 in_=lin[:, n, 0, :, :],
             )
 
-        with ExitStack() as main_loop:
-            weights = main_loop.enter_context(tc.tile_pool(name="weights", bufs=1))
-            h1_raw_pool = main_loop.enter_context(tc.tile_pool(name="h1_raw", bufs=4))
-            stage = main_loop.enter_context(tc.tile_pool(name="stage", bufs=2))
-            gates = main_loop.enter_context(tc.tile_pool(name="gates", bufs=2))
+        regroup_h1(0)
+        quantise_h1(0)
+        w_codes, w_scales = {}, {}
 
-            def load_h1(n):
-                h1_raw = h1_raw_pool.tile([P, PACK * K], BF16)
-                nc.sync.dma_start(
-                    out=h1_raw[:],
-                    in_=h1[n * ROWS : (n + 1) * ROWS, :].rearrange("(r j) k -> r (j k)", j=PACK),
-                )
-                return h1_raw
+        def prepare_gate(g):
+            w_grouped = regroup_512_rows(nc, psum_t, stage, identity[:], w_raw[g][:], nc.vector.tensor_copy)
+            w_codes[g] = consts.tile([P, ROWS], U32, name="w_codes%d" % g, align_bytes=64)
+            w_scales[g] = consts.tile([P, ROWS], U8, name="w_scales%d" % g, align_bytes=64)
+            nc.vector.quantize_mx(out=w_codes[g][:].bitcast(FP8X4), scales=w_scales[g][:], in_=w_grouped[:])
 
-            h1_raw = {0: load_h1(0)}
-            w_raw = {}
-            for g in GATE_ORDER:
-                w_raw[g] = weights.tile([P, PACK * K], BF16, name="w_raw%d" % g)
-                nc.sync.dma_start(
-                    out=w_raw[g][:],
-                    in_=W_ih1[g * HID : (g + 1) * HID, :].rearrange("(m t) k -> m (t k)", t=PACK),
-                )
-            head_raw = weights.tile([P, PACK * K], BF16)
-            head_raw_tiles = head_raw[:].rearrange("r (a k) -> r a k", a=PACK)
-            nc.sync.dma_start(out=head_raw_tiles[:, 0:2, :], in_=mu_W.rearrange("(a r) k -> r a k", a=2))
-            nc.sync.dma_start(out=head_raw_tiles[:, 2:4, :], in_=sig_W.rearrange("(a r) k -> r a k", a=2))
+        prepare_gate(GATE_I)
+        prepare_gate(GATE_G)
 
-            bias_parts = []
-            for vector in (hh_gates, b_ih1, b_hh1):
-                part = consts.tile([P, NG, PACK], BF16, name="bias_part%d" % len(bias_parts))
-                nc.scalar.dma_start(out=part[:], in_=vector.rearrange("(g m t) -> m g t", g=NG, t=PACK))
-                bias_parts.append(part)
-            c_init_bf = consts.tile([P, PACK], BF16)
-            nc.scalar.dma_start(out=c_init_bf[:], in_=c_init.rearrange("(m t) -> m t", t=PACK))
-            gate_bias = consts.tile([P, NG, PACK], F32)
-            nc.vector.tensor_tensor(out=gate_bias[:], in0=bias_parts[1][:], in1=bias_parts[2][:], op=ALU.add)
-            nc.vector.tensor_tensor(out=gate_bias[:], in0=gate_bias[:], in1=bias_parts[0][:], op=ALU.add)
-            c_init_f = consts.tile([P, PACK], F32)
-            nc.vector.tensor_copy(out=c_init_f[:], in_=c_init_bf[:])
+        head_codes = consts.tile([P, ROWS], U32, align_bytes=64)
+        head_scales = consts.tile([P, ROWS], U8, align_bytes=64)
+        spread = consts.tile([P, 4 * OUT], F32)
+        head_bias = spread[:, 0 : 2 * OUT].rearrange("r (h c) -> r h c", h=2)
+        ln_g_all = spread[:, 2 * OUT : 3 * OUT]
+        ln_b_all = spread[:, 3 * OUT : 4 * OUT]
 
-            head_rows = weights.tile([P, 4 * OUT], BF16)
-            nc.vector.memset(head_rows[:], 0.0)
-            for slot, vector in enumerate((mu_b, sig_b, ln_g, ln_b)):
-                nc.scalar.dma_start(out=head_rows[0:1, slot * OUT : (slot + 1) * OUT], in_=vector.unsqueeze(0))
-            ones = weights.tile([P, P], BF16)
-            nc.vector.memset(ones[:], 1.0)
-            spread = consts.tile([P, 4 * OUT], F32)
+        def prepare_heads():
+            head_grouped = regroup_512_rows(nc, psum_t, stage, identity[:], head_raw[:], nc.vector.tensor_copy)
             for half in range(2):
                 cols = slice(half * 2 * OUT, (half + 1) * 2 * OUT)
                 spread_ps = psum_head.tile([P, 2 * OUT], F32, tag="head")
                 nc.tensor.matmul(out=spread_ps[:], lhsT=ones[:], rhs=head_rows[:, cols], start=True, stop=True)
                 nc.vector.tensor_copy(out=spread[:, cols], in_=spread_ps[:])
-            head_bias = spread[:, 0 : 2 * OUT].rearrange("r (h c) -> r h c", h=2)
-            ln_g_all = spread[:, 2 * OUT : 3 * OUT]
-            ln_b_all = spread[:, 3 * OUT : 4 * OUT]
+            nc.vector.quantize_mx(out=head_codes[:].bitcast(FP8X4), scales=head_scales[:], in_=head_grouped[:])
 
-            def quantise_h1(n):
-                codes = stage.tile([P, ROWS], U32, name="h1_codes", align_bytes=64)
-                scales = stage.tile([P, ROWS], U8, name="h1_scales", align_bytes=64)
-                quantise_512_rows(nc, psum_t, stage, identity[:], h1_raw[n][:], codes[:], scales[:])
-                return codes, scales
+        def due(stage_of_block, n):
+            if 0 <= n < NBLK:
+                stage_of_block(n)
 
-            h1_q = {0: quantise_h1(0)}
-            w_codes, w_scales = {}, {}
-            for g in GATE_ORDER:
-                w_codes[g] = weights.tile([P, ROWS], U32, name="w_codes%d" % g, align_bytes=64)
-                w_scales[g] = weights.tile([P, ROWS], U8, name="w_scales%d" % g, align_bytes=64)
-                quantise_512_rows(nc, psum_t, stage, identity[:], w_raw[g][:], w_codes[g][:], w_scales[g][:])
-            head_codes = weights.tile([P, ROWS], U32, align_bytes=64)
-            head_scales = weights.tile([P, ROWS], U8, align_bytes=64)
-            quantise_512_rows(nc, psum_t, stage, identity[:], head_raw[:], head_codes[:], head_scales[:])
-            for n in range(1, 4):
-                h1_raw[n] = load_h1(n)
+        with tc.tile_pool(name="gates", bufs=2) as gates:
+            for n in range(NBLK + 1):
+                if n < NBLK:
+                    gate(n, GATE_I)
+                if n == 0:
+                    prepare_gate(GATE_F)
+                due(regroup_h1, n + 1)
+                due(hidden, n - 1)
+                if n < NBLK:
+                    due(normalise_first_half, n - 2)
+                due(quantise_hidden, n - 1)
+                due(quantise_h1, n + 1)
+                if n < NBLK:
+                    gate(n, GATE_G)
+                if n == 0:
+                    prepare_gate(GATE_O)
+                due(heads, n - 1)
+                due(clamp, n - 1)
+                due(input_times_candidate, n)
+                if n < NBLK:
+                    gate(n, GATE_F)
+                due(new_cell, n)
+                if n == 0:
+                    prepare_heads()
+                if n < NBLK:
+                    gate(n, GATE_O)
+                if n < NBLK:
+                    due(normalise_second_half, n - 2)
+                due(tanh_cell, n)
 
+        for n in range(NBLK - 2, NBLK):
+            normalise_first_half(n)
+            normalise_second_half(n)
+
+        with tc.manual_schedule():
             for n in range(NBLK):
-                if n + 4 < NBLK:
-                    h1_raw[n + 4] = load_h1(n + 4)
-                if n + 1 < NBLK:
-                    h1_q[n + 1] = quantise_h1(n + 1)
-                codes, scales = h1_q[n]
-
-                act = {}
-                for g in GATE_ORDER:
-                    act[g] = gates.tile([P, PACK, ROWS], F32, name="gate%d" % g)
-                    for t in range(PACK):
-                        units = slice(t * P, (t + 1) * P)
-                        gate_ps = psum_gate.tile([P, ROWS], F32, tag="gate")
-                        nc.tensor.matmul_mx(
-                            out=gate_ps[:],
-                            lhsT=w_codes[g][:, units].bitcast(FP8X4), lhsT_scale=w_scales[g][:, units],
-                            rhs=codes[:].bitcast(FP8X4), rhs_scale=scales[:],
-                            start=True, stop=True,
-                        )
-                        nc.scalar.activation(
-                            out=act[g][:, t, :], in_=gate_ps[:],
-                            func=ACT.Tanh if g == GATE_G else ACT.Sigmoid,
-                            bias=gate_bias[:, g, t : t + 1], scale=1.0,
-                        )
-                        if g == GATE_G:
-                            nc.gpsimd.tensor_tensor(
-                                out=act[GATE_I][:, t, :], in0=act[GATE_I][:, t, :], in1=act[GATE_G][:, t, :], op=ALU.mult
-                            )
-                    if g == GATE_F:
-                        for t in range(PACK):
-                            nc.vector.scalar_tensor_tensor(
-                                out=act[GATE_F][:, t, :], in0=act[GATE_F][:, t, :], scalar=c_init_f[:, t : t + 1],
-                                in1=act[GATE_I][:, t, :], op0=ALU.mult, op1=ALU.add,
-                            )
-                cell = act[GATE_F]
-                nc.scalar.activation(out=cell[:], in_=cell[:], func=ACT.Tanh)
-
-                h2 = stage.tile([P, ROWS * PACK], BF16, align_bytes=64)
-                nc.vector.tensor_tensor(
-                    out=h2[:].rearrange("m (c i t) -> m c t i", i=4, t=PACK),
-                    in0=act[GATE_O][:].rearrange("m t (c i) -> m c t i", i=4),
-                    in1=cell[:].rearrange("m t (c i) -> m c t i", i=4),
-                    op=ALU.mult,
-                )
-                h2_codes = stage.tile([P, ROWS], U32, align_bytes=64)
-                h2_scales = stage.tile([P, ROWS], U8, align_bytes=64)
-                nc.vector.quantize_mx(out=h2_codes[:].bitcast(FP8X4), scales=h2_scales[:], in_=h2[:])
-
-                stats = norm.tile([P, PACK, 6], F32)
-                for j in range(PACK):
-                    rows = slice(j * P, (j + 1) * P)
-                    head_ps = psum_head.tile([P, 2 * OUT], F32, tag="head")
-                    nc.tensor.matmul_mx(
-                        out=head_ps[:],
-                        lhsT=h2_codes[:, rows].bitcast(FP8X4), lhsT_scale=h2_scales[:, rows],
-                        rhs=head_codes[:].bitcast(FP8X4), rhs_scale=head_scales[:],
-                        start=True, stop=True,
-                    )
-                    nc.vector.tensor_tensor(
-                        out=lin[:, n, :, j, :], in0=head_ps[:].rearrange("r (h c) -> r h c", h=2), in1=head_bias,
-                        op=ALU.add,
-                    )
-                    nc.vector.bn_stats(out=stats[:, j, :], in_=lin[:, n, 0, j, :])
-                    nc.vector.bn_aggr(out=mean_var[:, n, j, :], in_=stats[:, j, :])
-                nc.vector.tensor_scalar_add(out=var_eps[:, n, :], in0=mean_var[:, n, :, 1], scalar1=LN_EPS)
-                nc.gpsimd.tensor_tensor(out=rstd[:, n, :], in0=var_eps[:, n, :], in1=minus_half[:], op=ALU.pow)
-                if n >= NORM_LAG:
-                    normalise(n - NORM_LAG)
-
-        with tc.tile_pool(name="softplus", bufs=NBLK) as softplus:
-            exps = []
+                nc.scalar.activation(out=exps[n][:], in_=exps[n][:], func=ACT.Exp)
             for n in range(NBLK):
                 v = lin[:, n, 1, :, :].rearrange("r j c -> r (j c)")
-                e = softplus.tile([P, PACK * OUT], F32)
-                nc.vector.tensor_scalar_min(out=e[:], in0=v, scalar1=SOFTPLUS_LINEAR_FROM)
-                nc.scalar.activation(out=e[:], in_=e[:], func=ACT.Exp)
-                exps.append(e)
-            for n in range(NBLK - NORM_LAG, NBLK):
-                normalise(n)
-            for n in range(NBLK):
-                v = lin[:, n, 1, :, :].rearrange("r j c -> r (j c)")
-                e = exps[n]
-                nc.scalar.activation(out=e[:], in_=e[:], func=ACT.Ln, bias=1.0, scale=1.0)
+                nc.scalar.activation(out=exps[n][:], in_=exps[n][:], func=ACT.Ln, bias=1.0, scale=1.0)
                 nc.vector.scalar_tensor_tensor(
-                    out=v, in0=e[:], scalar=SIG_MIN, in1=v, op0=ALU.add, op1=ALU.max,
+                    out=v, in0=exps[n][:], scalar=SIG_MIN, in1=v, op0=ALU.add, op1=ALU.max,
                 )
                 nc.sync.dma_start(
                     out=out_1[n * ROWS : (n + 1) * ROWS, :].rearrange("(r j) c -> r j c", j=PACK),

@@ -100,13 +100,13 @@ def tile_rdecommunicationlstm_pb_t_kernel(
         minus_half = consts.tile([P, PACK], F32)
         nc.vector.memset(minus_half[:], -0.5)
         gate_bias = consts.tile([P, NG, PACK], F32)
-        nc.vector.tensor_tensor(out=gate_bias[:], in0=bias_parts[1][:], in1=bias_parts[2][:], op=ALU.add)
-        nc.vector.tensor_tensor(out=gate_bias[:], in0=gate_bias[:], in1=bias_parts[0][:], op=ALU.add)
+        nc.gpsimd.tensor_tensor(out=gate_bias[:], in0=bias_parts[1][:], in1=bias_parts[2][:], op=ALU.add)
+        nc.gpsimd.tensor_tensor(out=gate_bias[:], in0=gate_bias[:], in1=bias_parts[0][:], op=ALU.add)
         c_init_f = consts.tile([P, PACK], F32)
-        nc.vector.tensor_copy(out=c_init_f[:], in_=c_init_bf[:])
+        nc.gpsimd.tensor_copy(out=c_init_f[:], in_=c_init_bf[:])
 
         lin = consts.tile([P, NBLK, 2, PACK, OUT], F32)
-        mean_var = consts.tile([P, NBLK, PACK, 2], F32)
+        stats = consts.tile([P, NBLK, 2, 2, 3], F32)
         var_eps = consts.tile([P, NBLK, PACK], F32)
         rstd = consts.tile([P, NBLK, PACK], F32)
 
@@ -171,7 +171,13 @@ def tile_rdecommunicationlstm_pb_t_kernel(
 
         def heads(n):
             codes, scales = h2_q[n]
-            stats = stage.tile([P, PACK, 6], F32, name="stats")
+
+            def row_stats(h):
+                nc.vector.bn_stats(
+                    out=stats[:, n, h, :, :].rearrange("r e s -> r (e s)"),
+                    in_=lin[:, n, 0, 2 * h : 2 * h + 2, :].rearrange("r e c -> r c e"),
+                )
+
             for j in range(PACK):
                 rows = slice(j * P, (j + 1) * P)
                 head_ps = psum_head.tile([P, 2 * OUT], F32, tag="head")
@@ -185,9 +191,14 @@ def tile_rdecommunicationlstm_pb_t_kernel(
                     out=lin[:, n, :, j, :], in0=head_ps[:].rearrange("r (h c) -> r h c", h=2), in1=head_bias,
                     op=ALU.add,
                 )
-                nc.vector.bn_stats(out=stats[:, j, :], in_=lin[:, n, 0, j, :])
-                nc.vector.bn_aggr(out=mean_var[:, n, j, :], in_=stats[:, j, :])
-            nc.vector.tensor_scalar_add(out=var_eps[:, n, :], in0=mean_var[:, n, :, 1], scalar1=LN_EPS)
+                if j == 2:
+                    row_stats(0)
+            clamp(n)
+            row_stats(1)
+            nc.gpsimd.tensor_scalar(
+                out=var_eps[:, n, :], in0=stats[:, n, :, :, 2].rearrange("r h e -> r (h e)"),
+                scalar1=1.0 / OUT, scalar2=LN_EPS, op0=ALU.mult, op1=ALU.add,
+            )
             nc.gpsimd.tensor_tensor(out=rstd[:, n, :], in0=var_eps[:, n, :], in1=minus_half[:], op=ALU.pow)
 
         def clamp(n):
@@ -198,13 +209,13 @@ def tile_rdecommunicationlstm_pb_t_kernel(
 
         def normalise(n, tiles):
             for j in tiles:
-                centred = stage.tile([P, OUT], F32, name="centred")
                 nc.vector.scalar_tensor_tensor(
-                    out=centred[:], in0=lin[:, n, 0, j, :], scalar=mean_var[:, n, j, 0:1], in1=ln_g_all,
-                    op0=ALU.subtract, op1=ALU.mult,
+                    out=lin[:, n, 0, j, :], in0=lin[:, n, 0, j, :], scalar=stats[:, n, j // 2, j % 2, 1:2],
+                    in1=ln_g_all, op0=ALU.subtract, op1=ALU.mult,
                 )
+            for j in tiles:
                 nc.vector.scalar_tensor_tensor(
-                    out=lin[:, n, 0, j, :], in0=centred[:], scalar=rstd[:, n, j : j + 1], in1=ln_b_all,
+                    out=lin[:, n, 0, j, :], in0=lin[:, n, 0, j, :], scalar=rstd[:, n, j : j + 1], in1=ln_b_all,
                     op0=ALU.mult, op1=ALU.add,
                 )
 
@@ -268,7 +279,6 @@ def tile_rdecommunicationlstm_pb_t_kernel(
                 if n == 0:
                     prepare_gate(GATE_O)
                 due(heads, n - 1)
-                due(clamp, n - 1)
                 due(input_times_candidate, n)
                 if n < NBLK:
                     gate(n, GATE_F)

@@ -1,3 +1,4 @@
+import math
 from contextlib import ExitStack
 
 import concourse.mybir as mybir
@@ -22,27 +23,12 @@ GATE_I, GATE_F, GATE_G, GATE_O = 0, 1, 2, 3
 GATE_ORDER = (GATE_I, GATE_G, GATE_F, GATE_O)
 LN_EPS = 1e-5
 SIG_MIN = 1e-6
-SOFTPLUS_LINEAR_FROM = 32.0
+SIG_SCALE = math.exp(-SIG_MIN)
+SIG_FLOOR = 2.0**-62
 
-FILL_BLOCKS = 1
+CELL_ON_TENSOR = (2, 3)
 
 FLOPS = 2 * BATCH * HID * (NG * HID) + 2 * BATCH * HID * (2 * OUT)
-
-
-def regroup_512_rows(nc, psum, stage, identity, raw, copy_out):
-    words = raw.bitcast(F32).rearrange("r (a q u) -> r a u q", a=PACK, u=2)
-    grouped = stage.tile([P, ROWS * PACK], BF16, align_bytes=64)
-    grouped_words = grouped[:].bitcast(F32).rearrange("q (a r u) -> q a r u", a=PACK, u=2)
-    for half in range(2):
-        bank = psum.tile([P, 2, 2, P], F32, tag="transposed")
-        for a in range(2):
-            for u in range(2):
-                nc.tensor.transpose(bank[:, a, u, :], words[:, 2 * half + a, u, :], identity)
-        copy_out(
-            out=grouped_words[:, 2 * half : 2 * half + 2, :, :],
-            in_=bank[:].rearrange("q a u r -> q a r u"),
-        )
-    return grouped
 
 
 def tile_rdecommunicationlstm_pb_t_kernel(
@@ -53,10 +39,12 @@ def tile_rdecommunicationlstm_pb_t_kernel(
         consts = pools.enter_context(tc.tile_pool(name="consts", bufs=1))
         raw_pool = pools.enter_context(tc.tile_pool(name="raw", bufs=5))
         stage = pools.enter_context(tc.tile_pool(name="stage", bufs=2))
+        gates = pools.enter_context(tc.tile_pool(name="gates", bufs=2))
         softplus = pools.enter_context(tc.tile_pool(name="softplus", bufs=NBLK))
         psum_t = pools.enter_context(tc.psum_pool(name="psum_t", bufs=2))
         psum_gate = pools.enter_context(tc.psum_pool(name="psum_gate", bufs=4))
         psum_head = pools.enter_context(tc.psum_pool(name="psum_head", bufs=2))
+        pools.enter_context(tc.manual_schedule())
 
         def load_rows(source):
             raw = raw_pool.tile([P, PACK * K], BF16, name="raw")
@@ -84,7 +72,7 @@ def tile_rdecommunicationlstm_pb_t_kernel(
         nc.sync.dma_start(out=head_raw_tiles[:, 0:2, :], in_=mu_W.rearrange("(a r) k -> r a k", a=2))
         nc.sync.dma_start(out=head_raw_tiles[:, 2:4, :], in_=sig_W.rearrange("(a r) k -> r a k", a=2))
         head_rows = consts.tile([P, 4 * OUT], BF16)
-        nc.vector.memset(head_rows[:], 0.0)
+        nc.gpsimd.memset(head_rows[:], 0.0)
         for slot, vector in enumerate((mu_b, sig_b, ln_g, ln_b)):
             nc.sync.dma_start(out=head_rows[0:1, slot * OUT : (slot + 1) * OUT], in_=vector.unsqueeze(0))
         for n in range(2, NBLK):
@@ -104,33 +92,57 @@ def tile_rdecommunicationlstm_pb_t_kernel(
         nc.gpsimd.tensor_tensor(out=gate_bias[:], in0=gate_bias[:], in1=bias_parts[0][:], op=ALU.add)
         c_init_f = consts.tile([P, PACK], F32)
         nc.gpsimd.tensor_copy(out=c_init_f[:], in_=c_init_bf[:])
+        diag_c = {}
+        for t in CELL_ON_TENSOR:
+            diag_c[t] = consts.tile([P, P], F32, name="diag_c%d" % t)
+            nc.gpsimd.tensor_scalar(
+                out=diag_c[t][:], in0=identity[:], scalar1=c_init_f[:, t : t + 1], scalar2=None, op0=ALU.mult
+            )
 
         lin = consts.tile([P, NBLK, 2, PACK, OUT], F32)
         stats = consts.tile([P, NBLK, 2, 2, 3], F32)
         var_eps = consts.tile([P, NBLK, PACK], F32)
         rstd = consts.tile([P, NBLK, PACK], F32)
 
-        h1_grouped, h1_q, act, h2, h2_q, exps = {}, {}, {}, {}, {}, {}
+        def regroup(raw, copies):
+            words = raw[:].bitcast(F32).rearrange("r (a q u) -> r a u q", a=PACK, u=2)
+            grouped = stage.tile([P, ROWS * PACK], BF16, name="grouped", align_bytes=64)
+            grouped_words = grouped[:].bitcast(F32).rearrange("q (a r u) -> q a r u", a=PACK, u=2)
+            for half, copy_out in enumerate(copies):
+                bank = psum_t.tile([P, 2, 2, P], F32, tag="transposed")
+                for a in range(2):
+                    for u in range(2):
+                        nc.tensor.transpose(bank[:, a, u, :], words[:, 2 * half + a, u, :], identity[:])
+                copy_out(
+                    out=grouped_words[:, 2 * half : 2 * half + 2, :, :],
+                    in_=bank[:].rearrange("q a u r -> q a r u"),
+                )
+            return grouped
+
+        def quantise(values, pool, name):
+            codes = pool.tile([P, ROWS], U32, name=name + "_codes", align_bytes=64)
+            scales = pool.tile([P, ROWS], U8, name=name + "_scales", align_bytes=64)
+            nc.vector.quantize_mx(out=codes[:].bitcast(FP8X4), scales=scales[:], in_=values[:])
+            return codes, scales
+
+        on_vector, on_scalar = nc.vector.tensor_copy, nc.scalar.copy
+        h1_grouped, h1_q, w_grouped, w_q, act, h2, h2_q, sigs, cell_ps, head_ps = {}, {}, {}, {}, {}, {}, {}, {}, {}, {}
 
         def regroup_h1(n):
-            copy_out = nc.vector.tensor_copy if n < FILL_BLOCKS else nc.scalar.copy
-            h1_grouped[n] = regroup_512_rows(nc, psum_t, stage, identity[:], h1_raw[n][:], copy_out)
+            h1_grouped[n] = regroup(h1_raw[n], (on_scalar, on_scalar))
 
         def quantise_h1(n):
-            codes = stage.tile([P, ROWS], U32, name="h1_codes", align_bytes=64)
-            scales = stage.tile([P, ROWS], U8, name="h1_scales", align_bytes=64)
-            nc.vector.quantize_mx(out=codes[:].bitcast(FP8X4), scales=scales[:], in_=h1_grouped[n][:])
-            h1_q[n] = (codes, scales)
+            h1_q[n] = quantise(h1_grouped[n], stage, "h1")
 
         def gate(n, g):
-            codes, scales = h1_q[n]
+            (codes, scales), (w_codes, w_scales) = h1_q[n], w_q[g]
             act[n, g] = gates.tile([P, PACK, ROWS], F32, name="gate%d" % g)
             for t in range(PACK):
                 units = slice(t * P, (t + 1) * P)
                 gate_ps = psum_gate.tile([P, ROWS], F32, tag="gate")
                 nc.tensor.matmul_mx(
                     out=gate_ps[:],
-                    lhsT=w_codes[g][:, units].bitcast(FP8X4), lhsT_scale=w_scales[g][:, units],
+                    lhsT=w_codes[:, units].bitcast(FP8X4), lhsT_scale=w_scales[:, units],
                     rhs=codes[:].bitcast(FP8X4), rhs_scale=scales[:],
                     start=True, stop=True,
                 )
@@ -140,11 +152,22 @@ def tile_rdecommunicationlstm_pb_t_kernel(
                     bias=gate_bias[:, g, t : t + 1], scale=1.0,
                 )
 
-        def input_times_candidate(n):
-            nc.vector.tensor_tensor(out=act[n, GATE_I][:], in0=act[n, GATE_I][:], in1=act[n, GATE_G][:], op=ALU.mult)
+        def input_times_candidate(n, tiles):
+            nc.vector.tensor_tensor(
+                out=act[n, GATE_I][:, tiles, :], in0=act[n, GATE_I][:, tiles, :], in1=act[n, GATE_G][:, tiles, :],
+                op=ALU.mult,
+            )
 
-        def new_cell(n):
-            for t in range(PACK):
+        def new_cell(n, t):
+            if t in CELL_ON_TENSOR:
+                cell_ps[n, t] = psum_head.tile([P, ROWS], F32, name="head")
+                nc.tensor.matmul(
+                    out=cell_ps[n, t][:], lhsT=diag_c[t][:], rhs=act[n, GATE_F][:, t, :], start=True, stop=False
+                )
+                nc.tensor.matmul(
+                    out=cell_ps[n, t][:], lhsT=identity[:], rhs=act[n, GATE_I][:, t, :], start=False, stop=True
+                )
+            else:
                 nc.vector.scalar_tensor_tensor(
                     out=act[n, GATE_F][:, t, :], in0=act[n, GATE_F][:, t, :], scalar=c_init_f[:, t : t + 1],
                     in1=act[n, GATE_I][:, t, :], op0=ALU.mult, op1=ALU.add,
@@ -152,7 +175,8 @@ def tile_rdecommunicationlstm_pb_t_kernel(
 
         def tanh_cell(n):
             for t in range(PACK):
-                nc.scalar.activation(out=act[n, GATE_F][:, t, :], in_=act[n, GATE_F][:, t, :], func=ACT.Tanh)
+                cell = cell_ps[n, t][:] if t in CELL_ON_TENSOR else act[n, GATE_F][:, t, :]
+                nc.scalar.activation(out=act[n, GATE_F][:, t, :], in_=cell, func=ACT.Tanh)
 
         def hidden(n):
             h2[n] = stage.tile([P, ROWS * PACK], BF16, name="h2", align_bytes=64)
@@ -164,147 +188,144 @@ def tile_rdecommunicationlstm_pb_t_kernel(
             )
 
         def quantise_hidden(n):
-            codes = stage.tile([P, ROWS], U32, name="h2_codes", align_bytes=64)
-            scales = stage.tile([P, ROWS], U8, name="h2_scales", align_bytes=64)
-            nc.vector.quantize_mx(out=codes[:].bitcast(FP8X4), scales=scales[:], in_=h2[n][:])
-            h2_q[n] = (codes, scales)
+            h2_q[n] = quantise(h2[n], stage, "h2")
 
-        def heads(n):
+        def head_product(n, j):
             codes, scales = h2_q[n]
+            rows = slice(j * P, (j + 1) * P)
+            head_ps[n, j] = psum_head.tile([P, 2 * OUT], F32, name="head")
+            nc.tensor.matmul_mx(
+                out=head_ps[n, j][:],
+                lhsT=codes[:, rows].bitcast(FP8X4), lhsT_scale=scales[:, rows],
+                rhs=head_q[0][:].bitcast(FP8X4), rhs_scale=head_q[1][:],
+                start=True, stop=True,
+            )
 
-            def row_stats(h):
+        def head_sum(n, j):
+            nc.vector.tensor_tensor(
+                out=lin[:, n, :, j, :], in0=head_ps[n, j][:].rearrange("r (h c) -> r h c", h=2), in1=head_bias,
+                op=ALU.add,
+            )
+
+        def row_stats(n):
+            for h in range(2):
                 nc.vector.bn_stats(
                     out=stats[:, n, h, :, :].rearrange("r e s -> r (e s)"),
                     in_=lin[:, n, 0, 2 * h : 2 * h + 2, :].rearrange("r e c -> r c e"),
                 )
-
-            for j in range(PACK):
-                rows = slice(j * P, (j + 1) * P)
-                head_ps = psum_head.tile([P, 2 * OUT], F32, tag="head")
-                nc.tensor.matmul_mx(
-                    out=head_ps[:],
-                    lhsT=codes[:, rows].bitcast(FP8X4), lhsT_scale=scales[:, rows],
-                    rhs=head_codes[:].bitcast(FP8X4), rhs_scale=head_scales[:],
-                    start=True, stop=True,
-                )
-                nc.vector.tensor_tensor(
-                    out=lin[:, n, :, j, :], in0=head_ps[:].rearrange("r (h c) -> r h c", h=2), in1=head_bias,
-                    op=ALU.add,
-                )
-                if j == 2:
-                    row_stats(0)
-            clamp(n)
-            row_stats(1)
             nc.gpsimd.tensor_scalar(
                 out=var_eps[:, n, :], in0=stats[:, n, :, :, 2].rearrange("r h e -> r (h e)"),
                 scalar1=1.0 / OUT, scalar2=LN_EPS, op0=ALU.mult, op1=ALU.add,
             )
             nc.gpsimd.tensor_tensor(out=rstd[:, n, :], in0=var_eps[:, n, :], in1=minus_half[:], op=ALU.pow)
 
-        def clamp(n):
-            exps[n] = softplus.tile([P, PACK * OUT], F32, name="exps")
-            nc.vector.tensor_scalar_min(
-                out=exps[n][:], in0=lin[:, n, 1, :, :].rearrange("r j c -> r (j c)"), scalar1=SOFTPLUS_LINEAR_FROM
+        def sigmoid_spread(n, tiles=slice(0, PACK)):
+            if n not in sigs:
+                sigs[n] = softplus.tile([P, PACK, OUT], F32, name="sigs")
+            nc.scalar.activation(
+                out=sigs[n][:, tiles, :], in_=lin[:, n, 1, tiles, :], func=ACT.Sigmoid, bias=0.0, scale=-1.0
             )
 
-        def normalise(n, tiles):
-            for j in tiles:
+        def normalise(n):
+            for j in range(PACK):
                 nc.vector.scalar_tensor_tensor(
                     out=lin[:, n, 0, j, :], in0=lin[:, n, 0, j, :], scalar=stats[:, n, j // 2, j % 2, 1:2],
                     in1=ln_g_all, op0=ALU.subtract, op1=ALU.mult,
                 )
-            for j in tiles:
+            for j in range(PACK):
                 nc.vector.scalar_tensor_tensor(
                     out=lin[:, n, 0, j, :], in0=lin[:, n, 0, j, :], scalar=rstd[:, n, j : j + 1], in1=ln_b_all,
                     op0=ALU.mult, op1=ALU.add,
                 )
-
-        def normalise_first_half(n):
-            normalise(n, (0, 1))
-
-        def normalise_second_half(n):
-            normalise(n, (2, 3))
             nc.sync.dma_start(
                 out=out_0[n * ROWS : (n + 1) * ROWS, :].rearrange("(r j) c -> r j c", j=PACK),
                 in_=lin[:, n, 0, :, :],
             )
 
-        regroup_h1(0)
+        def softplus_log(n):
+            v = lin[:, n, 1, :, :]
+            nc.scalar.activation(
+                out=sigs[n][:], in_=sigs[n][:], func=ACT.Ln, bias=SIG_SCALE * SIG_FLOOR, scale=SIG_SCALE
+            )
+            nc.vector.scalar_tensor_tensor(
+                out=v, in0=sigs[n][:], scalar=-1.0, in1=v, op0=ALU.mult, op1=ALU.max,
+            )
+            nc.sync.dma_start(
+                out=out_1[n * ROWS : (n + 1) * ROWS, :].rearrange("(r j) c -> r j c", j=PACK), in_=v
+            )
+
+        h1_grouped[0] = regroup(h1_raw[0], (on_vector, on_scalar))
+        w_grouped[GATE_I] = regroup(w_raw[GATE_I], (on_vector, on_scalar))
         quantise_h1(0)
-        w_codes, w_scales = {}, {}
+        w_q[GATE_I] = quantise(w_grouped[GATE_I], consts, "w%d" % GATE_I)
 
         def prepare_gate(g):
-            w_grouped = regroup_512_rows(nc, psum_t, stage, identity[:], w_raw[g][:], nc.vector.tensor_copy)
-            w_codes[g] = consts.tile([P, ROWS], U32, name="w_codes%d" % g, align_bytes=64)
-            w_scales[g] = consts.tile([P, ROWS], U8, name="w_scales%d" % g, align_bytes=64)
-            nc.vector.quantize_mx(out=w_codes[g][:].bitcast(FP8X4), scales=w_scales[g][:], in_=w_grouped[:])
+            w_grouped[g] = regroup(w_raw[g], (on_vector, on_vector))
+            w_q[g] = quantise(w_grouped[g], consts, "w%d" % g)
 
-        prepare_gate(GATE_I)
         prepare_gate(GATE_G)
 
-        head_codes = consts.tile([P, ROWS], U32, align_bytes=64)
-        head_scales = consts.tile([P, ROWS], U8, align_bytes=64)
         spread = consts.tile([P, 4 * OUT], F32)
         head_bias = spread[:, 0 : 2 * OUT].rearrange("r (h c) -> r h c", h=2)
         ln_g_all = spread[:, 2 * OUT : 3 * OUT]
         ln_b_all = spread[:, 3 * OUT : 4 * OUT]
 
-        def prepare_heads():
-            head_grouped = regroup_512_rows(nc, psum_t, stage, identity[:], head_raw[:], nc.vector.tensor_copy)
-            for half in range(2):
-                cols = slice(half * 2 * OUT, (half + 1) * 2 * OUT)
-                spread_ps = psum_head.tile([P, 2 * OUT], F32, tag="head")
-                nc.tensor.matmul(out=spread_ps[:], lhsT=ones[:], rhs=head_rows[:, cols], start=True, stop=True)
-                nc.vector.tensor_copy(out=spread[:, cols], in_=spread_ps[:])
-            nc.vector.quantize_mx(out=head_codes[:].bitcast(FP8X4), scales=head_scales[:], in_=head_grouped[:])
+        for n in range(NBLK):
+            last = n - 1
+            gate(n, GATE_I)
+            if n == 0:
+                prepare_gate(GATE_F)
+            else:
+                hidden(last)
+                quantise_hidden(last)
+                if n + 1 < NBLK:
+                    quantise_h1(n + 1)
+            gate(n, GATE_G)
+            if n == 0:
+                prepare_gate(GATE_O)
+            else:
+                head_product(last, 0)
+                head_product(last, 1)
+            gate(n, GATE_F)
+            if n > 0:
+                head_sum(last, 0)
+                head_product(last, 2)
+                head_sum(last, 1)
+                head_product(last, 3)
+                head_sum(last, 2)
+                head_sum(last, 3)
+                row_stats(last)
+            input_times_candidate(n, slice(2, 4))
+            input_times_candidate(n, slice(0, 2))
+            gate(n, GATE_O)
+            if n > 0:
+                sigmoid_spread(last)
+            for ahead in (1, 2) if n == 0 else (n + 2,):
+                if ahead < NBLK:
+                    regroup_h1(ahead)
+            for t in range(PACK):
+                new_cell(n, t)
+            tanh_cell(n)
+            if n == 0:
+                quantise_h1(1)
+                head_q = quantise(regroup(head_raw, (on_vector, on_vector)), consts, "head")
+                for half in range(2):
+                    cols = slice(half * 2 * OUT, (half + 1) * 2 * OUT)
+                    spread_ps = psum_head.tile([P, 2 * OUT], F32, name="head")
+                    nc.tensor.matmul(out=spread_ps[:], lhsT=ones[:], rhs=head_rows[:, cols], start=True, stop=True)
+                    nc.vector.tensor_copy(out=spread[:, cols], in_=spread_ps[:])
+            else:
+                normalise(last)
 
-        def due(stage_of_block, n):
-            if 0 <= n < NBLK:
-                stage_of_block(n)
-
-        with tc.tile_pool(name="gates", bufs=2) as gates:
-            for n in range(NBLK + 1):
-                if n < NBLK:
-                    gate(n, GATE_I)
-                if n == 0:
-                    prepare_gate(GATE_F)
-                due(regroup_h1, n + 1)
-                due(hidden, n - 1)
-                if n < NBLK:
-                    due(normalise_first_half, n - 2)
-                due(quantise_hidden, n - 1)
-                due(quantise_h1, n + 1)
-                if n < NBLK:
-                    gate(n, GATE_G)
-                if n == 0:
-                    prepare_gate(GATE_O)
-                due(heads, n - 1)
-                due(input_times_candidate, n)
-                if n < NBLK:
-                    gate(n, GATE_F)
-                due(new_cell, n)
-                if n == 0:
-                    prepare_heads()
-                if n < NBLK:
-                    gate(n, GATE_O)
-                if n < NBLK:
-                    due(normalise_second_half, n - 2)
-                due(tanh_cell, n)
-
-        for n in range(NBLK - 2, NBLK):
-            normalise_first_half(n)
-            normalise_second_half(n)
-
-        with tc.manual_schedule():
-            for n in range(NBLK):
-                nc.scalar.activation(out=exps[n][:], in_=exps[n][:], func=ACT.Exp)
-            for n in range(NBLK):
-                v = lin[:, n, 1, :, :].rearrange("r j c -> r (j c)")
-                nc.scalar.activation(out=exps[n][:], in_=exps[n][:], func=ACT.Ln, bias=1.0, scale=1.0)
-                nc.vector.scalar_tensor_tensor(
-                    out=v, in0=exps[n][:], scalar=SIG_MIN, in1=v, op0=ALU.add, op1=ALU.max,
-                )
-                nc.sync.dma_start(
-                    out=out_1[n * ROWS : (n + 1) * ROWS, :].rearrange("(r j) c -> r j c", j=PACK),
-                    in_=lin[:, n, 1, :, :],
-                )
+        last = NBLK - 1
+        hidden(last)
+        quantise_hidden(last)
+        for j in range(PACK):
+            head_product(last, j)
+            head_sum(last, j)
+            sigmoid_spread(last, slice(j, j + 1))
+        row_stats(last)
+        for n in range(NBLK):
+            softplus_log(n)
+            if n == 0:
+                normalise(last)

@@ -213,7 +213,9 @@ def tile_rdecommunicationlstm_pb_t_kernel(
                     out=stats[:, n, h, :, :].rearrange("r e s -> r (e s)"),
                     in_=lin[:, n, 0, 2 * h : 2 * h + 2, :].rearrange("r e c -> r c e"),
                 )
-            nc.gpsimd.tensor_scalar(
+
+        def row_rstd(n):
+            nc.vector.tensor_scalar(
                 out=var_eps[:, n, :], in0=stats[:, n, :, :, 2].rearrange("r h e -> r (h e)"),
                 scalar1=1.0 / OUT, scalar2=LN_EPS, op0=ALU.mult, op1=ALU.add,
             )
@@ -287,6 +289,8 @@ def tile_rdecommunicationlstm_pb_t_kernel(
                 head_product(last, 0)
                 head_product(last, 1)
             gate(n, GATE_F)
+            if n > 1:
+                row_rstd(n - 2)
             if n > 0:
                 head_sum(last, 0)
                 head_product(last, 2)
@@ -314,17 +318,20 @@ def tile_rdecommunicationlstm_pb_t_kernel(
                     spread_ps = psum_head.tile([P, 2 * OUT], F32, name="head")
                     nc.tensor.matmul(out=spread_ps[:], lhsT=ones[:], rhs=head_rows[:, cols], start=True, stop=True)
                     nc.vector.tensor_copy(out=spread[:, cols], in_=spread_ps[:])
-            else:
-                normalise(last)
+            elif n > 1:
+                normalise(n - 2)
 
         last = NBLK - 1
         hidden(last)
         quantise_hidden(last)
+        row_rstd(last - 1)
         for j in range(PACK):
             head_product(last, j)
             head_sum(last, j)
             sigmoid_spread(last, slice(j, j + 1))
         row_stats(last)
+        row_rstd(last)
+        normalise(last - 1)
         for n in range(NBLK):
             softplus_log(n)
             if n == 0:

@@ -26,7 +26,8 @@ SIG_MIN = 1e-6
 SIG_SCALE = math.exp(-SIG_MIN)
 SIG_FLOOR = 2.0**-62
 
-CELL_ON_TENSOR = (2, 3)
+OFF_VECTOR = (0, 1)
+ON_VECTOR = (2, 3)
 
 FLOPS = 2 * BATCH * HID * (NG * HID) + 2 * BATCH * HID * (2 * OUT)
 
@@ -46,9 +47,12 @@ def tile_rdecommunicationlstm_pb_t_kernel(
         psum_head = pools.enter_context(tc.psum_pool(name="psum_head", bufs=2))
         pools.enter_context(tc.manual_schedule())
 
-        def load_rows(source):
+        def load_rows(source, pieces=1):
             raw = raw_pool.tile([P, PACK * K], BF16, name="raw")
-            nc.sync.dma_start(out=raw[:], in_=source)
+            width = PACK * K // pieces
+            for piece in range(pieces):
+                cols = slice(piece * width, (piece + 1) * width)
+                nc.sync.dma_start(out=raw[:, cols], in_=source[:, cols])
             return raw
 
         def h1_rows(n):
@@ -62,10 +66,13 @@ def tile_rdecommunicationlstm_pb_t_kernel(
         c_init_bf = consts.tile([P, PACK], BF16)
         nc.scalar.dma_start(out=c_init_bf[:], in_=c_init.rearrange("(m t) -> m t", t=PACK))
 
-        h1_raw = {0: load_rows(h1_rows(0))}
+        h1_raw = {0: load_rows(h1_rows(0), pieces=2)}
         w_raw = {}
         for g in GATE_ORDER:
-            w_raw[g] = load_rows(W_ih1[g * HID : (g + 1) * HID, :].rearrange("(m t) k -> m (t k)", t=PACK))
+            w_raw[g] = load_rows(
+                W_ih1[g * HID : (g + 1) * HID, :].rearrange("(m t) k -> m (t k)", t=PACK),
+                pieces=2 if g == GATE_ORDER[0] else 1,
+            )
         h1_raw[1] = load_rows(h1_rows(1))
         head_raw = raw_pool.tile([P, PACK * K], BF16, name="raw")
         head_raw_tiles = head_raw[:].rearrange("r (a k) -> r a k", a=PACK)
@@ -93,7 +100,7 @@ def tile_rdecommunicationlstm_pb_t_kernel(
         c_init_f = consts.tile([P, PACK], F32)
         nc.gpsimd.tensor_copy(out=c_init_f[:], in_=c_init_bf[:])
         diag_c = {}
-        for t in CELL_ON_TENSOR:
+        for t in OFF_VECTOR:
             diag_c[t] = consts.tile([P, P], F32, name="diag_c%d" % t)
             nc.gpsimd.tensor_scalar(
                 out=diag_c[t][:], in0=identity[:], scalar1=c_init_f[:, t : t + 1], scalar2=None, op0=ALU.mult
@@ -119,25 +126,32 @@ def tile_rdecommunicationlstm_pb_t_kernel(
                 )
             return grouped
 
-        def quantise(values, pool, name):
+        def quantise(values, pool, name, pieces=1):
             codes = pool.tile([P, ROWS], U32, name=name + "_codes", align_bytes=64)
             scales = pool.tile([P, ROWS], U8, name=name + "_scales", align_bytes=64)
-            nc.vector.quantize_mx(out=codes[:].bitcast(FP8X4), scales=scales[:], in_=values[:])
+            width = ROWS // pieces
+            for piece in range(pieces):
+                cols = slice(piece * width, (piece + 1) * width)
+                nc.vector.quantize_mx(
+                    out=codes[:, cols].bitcast(FP8X4), scales=scales[:, cols],
+                    in_=values[:, piece * width * PACK : (piece + 1) * width * PACK],
+                )
             return codes, scales
 
         on_vector, on_scalar = nc.vector.tensor_copy, nc.scalar.copy
         h1_grouped, h1_q, w_grouped, w_q, act, h2, h2_q, sigs, cell_ps, head_ps = {}, {}, {}, {}, {}, {}, {}, {}, {}, {}
 
-        def regroup_h1(n):
-            h1_grouped[n] = regroup(h1_raw[n], (on_scalar, on_scalar))
+        def regroup_h1(n, copies):
+            h1_grouped[n] = regroup(h1_raw[n], copies)
 
         def quantise_h1(n):
             h1_q[n] = quantise(h1_grouped[n], stage, "h1")
 
-        def gate(n, g):
+        def gate(n, g, tiles=range(PACK)):
             (codes, scales), (w_codes, w_scales) = h1_q[n], w_q[g]
-            act[n, g] = gates.tile([P, PACK, ROWS], F32, name="gate%d" % g)
-            for t in range(PACK):
+            if (n, g) not in act:
+                act[n, g] = gates.tile([P, PACK, ROWS], F32, name="gate%d" % g)
+            for t in tiles:
                 units = slice(t * P, (t + 1) * P)
                 gate_ps = psum_gate.tile([P, ROWS], F32, tag="gate")
                 nc.tensor.matmul_mx(
@@ -152,30 +166,32 @@ def tile_rdecommunicationlstm_pb_t_kernel(
                     bias=gate_bias[:, g, t : t + 1], scale=1.0,
                 )
 
-        def input_times_candidate(n, tiles):
-            nc.vector.tensor_tensor(
+        def input_times_candidate(engine, n, tiles):
+            engine.tensor_tensor(
                 out=act[n, GATE_I][:, tiles, :], in0=act[n, GATE_I][:, tiles, :], in1=act[n, GATE_G][:, tiles, :],
                 op=ALU.mult,
             )
 
+        def open_cell(n, t):
+            cell_ps[n, t] = psum_head.tile([P, ROWS], F32, name="head")
+            nc.tensor.matmul(
+                out=cell_ps[n, t][:], lhsT=diag_c[t][:], rhs=act[n, GATE_F][:, t, :], start=True, stop=False
+            )
+
+        def close_cell(n, t):
+            nc.tensor.matmul(
+                out=cell_ps[n, t][:], lhsT=identity[:], rhs=act[n, GATE_I][:, t, :], start=False, stop=True
+            )
+
         def new_cell(n, t):
-            if t in CELL_ON_TENSOR:
-                cell_ps[n, t] = psum_head.tile([P, ROWS], F32, name="head")
-                nc.tensor.matmul(
-                    out=cell_ps[n, t][:], lhsT=diag_c[t][:], rhs=act[n, GATE_F][:, t, :], start=True, stop=False
-                )
-                nc.tensor.matmul(
-                    out=cell_ps[n, t][:], lhsT=identity[:], rhs=act[n, GATE_I][:, t, :], start=False, stop=True
-                )
-            else:
-                nc.vector.scalar_tensor_tensor(
-                    out=act[n, GATE_F][:, t, :], in0=act[n, GATE_F][:, t, :], scalar=c_init_f[:, t : t + 1],
-                    in1=act[n, GATE_I][:, t, :], op0=ALU.mult, op1=ALU.add,
-                )
+            nc.vector.scalar_tensor_tensor(
+                out=act[n, GATE_F][:, t, :], in0=act[n, GATE_F][:, t, :], scalar=c_init_f[:, t : t + 1],
+                in1=act[n, GATE_I][:, t, :], op0=ALU.mult, op1=ALU.add,
+            )
 
         def tanh_cell(n):
-            for t in range(PACK):
-                cell = cell_ps[n, t][:] if t in CELL_ON_TENSOR else act[n, GATE_F][:, t, :]
+            for t in ON_VECTOR + OFF_VECTOR:
+                cell = cell_ps[n, t][:] if t in OFF_VECTOR else act[n, GATE_F][:, t, :]
                 nc.scalar.activation(out=act[n, GATE_F][:, t, :], in_=cell, func=ACT.Tanh)
 
         def hidden(n):
@@ -257,15 +273,17 @@ def tile_rdecommunicationlstm_pb_t_kernel(
             )
 
         h1_grouped[0] = regroup(h1_raw[0], (on_vector, on_scalar))
-        w_grouped[GATE_I] = regroup(w_raw[GATE_I], (on_vector, on_scalar))
-        quantise_h1(0)
-        w_q[GATE_I] = quantise(w_grouped[GATE_I], consts, "w%d" % GATE_I)
+        h1_q[0] = quantise(h1_grouped[0], stage, "h1", pieces=2)
+        w_grouped[GATE_I] = regroup(w_raw[GATE_I], (on_scalar, on_scalar))
+        w_q[GATE_I] = quantise(w_grouped[GATE_I], consts, "w%d" % GATE_I, pieces=2)
 
         def prepare_gate(g):
             w_grouped[g] = regroup(w_raw[g], (on_vector, on_vector))
             w_q[g] = quantise(w_grouped[g], consts, "w%d" % g)
 
+        gate(0, GATE_I, (0, 1))
         prepare_gate(GATE_G)
+        gate(0, GATE_I, (2, 3))
 
         spread = consts.tile([P, 4 * OUT], F32)
         head_bias = spread[:, 0 : 2 * OUT].rearrange("r (h c) -> r h c", h=2)
@@ -274,10 +292,10 @@ def tile_rdecommunicationlstm_pb_t_kernel(
 
         for n in range(NBLK):
             last = n - 1
-            gate(n, GATE_I)
             if n == 0:
                 prepare_gate(GATE_F)
             else:
+                gate(n, GATE_I)
                 hidden(last)
                 quantise_hidden(last)
                 if n + 1 < NBLK:
@@ -289,6 +307,8 @@ def tile_rdecommunicationlstm_pb_t_kernel(
                 head_product(last, 0)
                 head_product(last, 1)
             gate(n, GATE_F)
+            if n == 0:
+                head_q = quantise(regroup(head_raw, (on_vector, on_vector)), consts, "head")
             if n > 1:
                 row_rstd(n - 2)
             if n > 0:
@@ -299,20 +319,26 @@ def tile_rdecommunicationlstm_pb_t_kernel(
                 head_sum(last, 2)
                 head_sum(last, 3)
                 row_stats(last)
-            input_times_candidate(n, slice(2, 4))
-            input_times_candidate(n, slice(0, 2))
+            for t in OFF_VECTOR:
+                input_times_candidate(nc.gpsimd, n, slice(t, t + 1))
+            input_times_candidate(nc.vector, n, slice(len(OFF_VECTOR), PACK))
+            for t in ON_VECTOR:
+                new_cell(n, t)
             gate(n, GATE_O)
             if n > 0:
                 sigmoid_spread(last)
-            for ahead in (1, 2) if n == 0 else (n + 2,):
-                if ahead < NBLK:
-                    regroup_h1(ahead)
-            for t in range(PACK):
-                new_cell(n, t)
+            if n == 0:
+                regroup_h1(1, (on_scalar, on_scalar))
+            elif n + 2 < NBLK:
+                regroup_h1(n + 2, (on_scalar, on_vector))
+            for t in OFF_VECTOR:
+                open_cell(n, t)
+            for t in OFF_VECTOR:
+                close_cell(n, t)
             tanh_cell(n)
             if n == 0:
                 quantise_h1(1)
-                head_q = quantise(regroup(head_raw, (on_vector, on_vector)), consts, "head")
+                regroup_h1(2, (on_vector, on_vector))
                 for half in range(2):
                     cols = slice(half * 2 * OUT, (half + 1) * 2 * OUT)
                     spread_ps = psum_head.tile([P, 2 * OUT], F32, name="head")

@@ -27,7 +27,6 @@ SIG_SCALE = math.exp(-SIG_MIN)
 SIG_FLOOR = 2.0**-62
 
 OFF_VECTOR = (0, 1)
-ON_VECTOR = (2, 3)
 
 FLOPS = 2 * BATCH * HID * (NG * HID) + 2 * BATCH * HID * (2 * OUT)
 
@@ -138,7 +137,7 @@ def tile_rdecommunicationlstm_pb_t_kernel(
                 )
             return codes, scales
 
-        on_vector, on_scalar = nc.vector.tensor_copy, nc.scalar.copy
+        copy_on_vector, copy_on_scalar = nc.vector.tensor_copy, nc.scalar.copy
         h1_grouped, h1_q, w_grouped, w_q, act, h2, h2_q, sigs, cell_ps, head_ps = {}, {}, {}, {}, {}, {}, {}, {}, {}, {}
 
         def regroup_h1(n, copies):
@@ -189,10 +188,8 @@ def tile_rdecommunicationlstm_pb_t_kernel(
                 in1=act[n, GATE_I][:, t, :], op0=ALU.mult, op1=ALU.add,
             )
 
-        def tanh_cell(n):
-            for t in ON_VECTOR + OFF_VECTOR:
-                cell = cell_ps[n, t][:] if t in OFF_VECTOR else act[n, GATE_F][:, t, :]
-                nc.scalar.activation(out=act[n, GATE_F][:, t, :], in_=cell, func=ACT.Tanh)
+        def tanh_cell(n, t, cell):
+            nc.scalar.activation(out=act[n, GATE_F][:, t, :], in_=cell, func=ACT.Tanh)
 
         def hidden(n):
             h2[n] = stage.tile([P, ROWS * PACK], BF16, name="h2", align_bytes=64)
@@ -272,13 +269,13 @@ def tile_rdecommunicationlstm_pb_t_kernel(
                 out=out_1[n * ROWS : (n + 1) * ROWS, :].rearrange("(r j) c -> r j c", j=PACK), in_=v
             )
 
-        h1_grouped[0] = regroup(h1_raw[0], (on_vector, on_scalar))
+        h1_grouped[0] = regroup(h1_raw[0], (copy_on_vector, copy_on_scalar))
         h1_q[0] = quantise(h1_grouped[0], stage, "h1", pieces=2)
-        w_grouped[GATE_I] = regroup(w_raw[GATE_I], (on_scalar, on_scalar))
+        w_grouped[GATE_I] = regroup(w_raw[GATE_I], (copy_on_scalar, copy_on_scalar))
         w_q[GATE_I] = quantise(w_grouped[GATE_I], consts, "w%d" % GATE_I, pieces=2)
 
         def prepare_gate(g):
-            w_grouped[g] = regroup(w_raw[g], (on_vector, on_vector))
+            w_grouped[g] = regroup(w_raw[g], (copy_on_vector, copy_on_vector))
             w_q[g] = quantise(w_grouped[g], consts, "w%d" % g)
 
         gate(0, GATE_I, (0, 1))
@@ -292,60 +289,66 @@ def tile_rdecommunicationlstm_pb_t_kernel(
 
         for n in range(NBLK):
             last = n - 1
+            on_tensor = OFF_VECTOR[:1] if n == 0 else OFF_VECTOR
+            on_vector_cells = [t for t in range(PACK) if t not in on_tensor]
             if n == 0:
                 prepare_gate(GATE_F)
             else:
                 gate(n, GATE_I)
                 hidden(last)
                 quantise_hidden(last)
-                if n + 1 < NBLK:
+                if 1 < n < NBLK - 1:
                     quantise_h1(n + 1)
             gate(n, GATE_G)
             if n == 0:
                 prepare_gate(GATE_O)
+                gate(n, GATE_F)
+                head_q = quantise(regroup(head_raw, (copy_on_vector, copy_on_vector)), consts, "head")
             else:
                 head_product(last, 0)
                 head_product(last, 1)
-            gate(n, GATE_F)
-            if n == 0:
-                head_q = quantise(regroup(head_raw, (on_vector, on_vector)), consts, "head")
-            if n > 1:
-                row_rstd(n - 2)
-            if n > 0:
+                if n > 1:
+                    row_rstd(n - 2)
+                gate(n, GATE_F, (0, 1))
                 head_sum(last, 0)
                 head_product(last, 2)
                 head_sum(last, 1)
                 head_product(last, 3)
+                gate(n, GATE_F, (2, 3))
                 head_sum(last, 2)
                 head_sum(last, 3)
                 row_stats(last)
             for t in OFF_VECTOR:
                 input_times_candidate(nc.gpsimd, n, slice(t, t + 1))
             input_times_candidate(nc.vector, n, slice(len(OFF_VECTOR), PACK))
-            for t in ON_VECTOR:
+            for t in on_vector_cells:
                 new_cell(n, t)
             gate(n, GATE_O)
             if n > 0:
                 sigmoid_spread(last)
             if n == 0:
-                regroup_h1(1, (on_scalar, on_scalar))
-            elif n + 2 < NBLK:
-                regroup_h1(n + 2, (on_scalar, on_vector))
-            for t in OFF_VECTOR:
-                open_cell(n, t)
-            for t in OFF_VECTOR:
-                close_cell(n, t)
-            tanh_cell(n)
-            if n == 0:
-                quantise_h1(1)
-                regroup_h1(2, (on_vector, on_vector))
+                regroup_h1(1, (copy_on_scalar, copy_on_scalar))
                 for half in range(2):
                     cols = slice(half * 2 * OUT, (half + 1) * 2 * OUT)
-                    spread_ps = psum_head.tile([P, 2 * OUT], F32, name="head")
+                    spread_ps = psum_gate.tile([P, 2 * OUT], F32, tag="gate")
                     nc.tensor.matmul(out=spread_ps[:], lhsT=ones[:], rhs=head_rows[:, cols], start=True, stop=True)
                     nc.vector.tensor_copy(out=spread[:, cols], in_=spread_ps[:])
-            elif n > 1:
+                quantise_h1(1)
+            elif n == 1:
+                regroup_h1(2, (copy_on_vector, copy_on_vector))
+                quantise_h1(2)
+            for t in on_tensor:
+                open_cell(n, t)
+            for t in on_tensor:
+                close_cell(n, t)
+            for t in on_vector_cells:
+                tanh_cell(n, t, act[n, GATE_F][:, t, :])
+            for t in on_tensor:
+                tanh_cell(n, t, cell_ps[n, t][:])
+            if n > 1:
                 normalise(n - 2)
+            if 0 < n < NBLK - 2:
+                regroup_h1(n + 2, (copy_on_vector, copy_on_vector))
 
         last = NBLK - 1
         hidden(last)

@@ -26,6 +26,7 @@ SIG_MIN = 1e-6
 SIG_SCALE = math.exp(-SIG_MIN)
 SIG_FLOOR = 2.0**-62
 
+PRODUCT_ON_GPSIMD = (0, 1, 2)
 OFF_VECTOR = (0, 1)
 
 FLOPS = 2 * BATCH * HID * (NG * HID) + 2 * BATCH * HID * (2 * OUT)
@@ -110,41 +111,58 @@ def tile_rdecommunicationlstm_pb_t_kernel(
         var_eps = consts.tile([P, NBLK, PACK], F32)
         rstd = consts.tile([P, NBLK, PACK], F32)
 
-        def regroup(raw, copies):
-            words = raw[:].bitcast(F32).rearrange("r (a q u) -> r a u q", a=PACK, u=2)
-            grouped = stage.tile([P, ROWS * PACK], BF16, name="grouped", align_bytes=64)
-            grouped_words = grouped[:].bitcast(F32).rearrange("q (a r u) -> q a r u", a=PACK, u=2)
-            for half, copy_out in enumerate(copies):
-                bank = psum_t.tile([P, 2, 2, P], F32, tag="transposed")
-                for a in range(2):
-                    for u in range(2):
-                        nc.tensor.transpose(bank[:, a, u, :], words[:, 2 * half + a, u, :], identity[:])
-                copy_out(
-                    out=grouped_words[:, 2 * half : 2 * half + 2, :, :],
-                    in_=bank[:].rearrange("q a u r -> q a r u"),
-                )
-            return grouped
+        def grouped_tile():
+            return stage.tile([P, ROWS * PACK], BF16, name="grouped", align_bytes=64)
 
-        def quantise(values, pool, name, pieces=1):
+        def transpose_half(raw, half):
+            words = raw[:].bitcast(F32).rearrange("r (a q u) -> r a u q", a=PACK, u=2)
+            bank = psum_t.tile([P, 2, 2, P], F32, tag="transposed")
+            for a in range(2):
+                for u in range(2):
+                    nc.tensor.transpose(bank[:, a, u, :], words[:, 2 * half + a, u, :], identity[:])
+            return bank
+
+        def copy_half(bank, grouped, half, copy_out):
+            grouped_words = grouped[:].bitcast(F32).rearrange("q (a r u) -> q a r u", a=PACK, u=2)
+            copy_out(
+                out=grouped_words[:, 2 * half : 2 * half + 2, :, :],
+                in_=bank[:].rearrange("q a u r -> q a r u"),
+            )
+
+        def operand(pool, name):
             codes = pool.tile([P, ROWS], U32, name=name + "_codes", align_bytes=64)
             scales = pool.tile([P, ROWS], U8, name=name + "_scales", align_bytes=64)
-            width = ROWS // pieces
-            for piece in range(pieces):
-                cols = slice(piece * width, (piece + 1) * width)
-                nc.vector.quantize_mx(
-                    out=codes[:, cols].bitcast(FP8X4), scales=scales[:, cols],
-                    in_=values[:, piece * width * PACK : (piece + 1) * width * PACK],
-                )
             return codes, scales
 
-        copy_on_vector, copy_on_scalar = nc.vector.tensor_copy, nc.scalar.copy
-        h1_grouped, h1_q, w_grouped, w_q, act, h2, h2_q, sigs, cell_ps, head_ps = {}, {}, {}, {}, {}, {}, {}, {}, {}, {}
+        def quantise(values, codes_scales, rows=slice(0, ROWS)):
+            codes, scales = codes_scales
+            nc.vector.quantize_mx(
+                out=codes[:, rows].bitcast(FP8X4), scales=scales[:, rows],
+                in_=values[:, PACK * rows.start : PACK * rows.stop],
+            )
 
-        def regroup_h1(n, copies):
-            h1_grouped[n] = regroup(h1_raw[n], copies)
+        def prepare(raw, copies, pool, name):
+            grouped, codes_scales = grouped_tile(), operand(pool, name)
+            for half, copy_out in enumerate(copies):
+                copy_half(transpose_half(raw, half), grouped, half, copy_out)
+                quantise(grouped, codes_scales, slice(half * ROWS // 2, (half + 1) * ROWS // 2))
+            return codes_scales
+
+        copy_on_vector, copy_on_scalar = nc.vector.tensor_copy, nc.scalar.copy
+        h1_banks, h1_grouped, h1_q, w_q = {}, {}, {}, {}
+        act, h2, h2_q, sigs, cell_ps, head_ps = {}, {}, {}, {}, {}, {}
+
+        def transpose_h1(n):
+            h1_banks[n] = [transpose_half(h1_raw[n], half) for half in range(2)]
+
+        def copy_h1(n, copy_out):
+            h1_grouped[n] = grouped_tile()
+            for half in range(2):
+                copy_half(h1_banks[n][half], h1_grouped[n], half, copy_out)
 
         def quantise_h1(n):
-            h1_q[n] = quantise(h1_grouped[n], stage, "h1")
+            h1_q[n] = operand(stage, "h1")
+            quantise(h1_grouped[n], h1_q[n])
 
         def gate(n, g, tiles=range(PACK)):
             (codes, scales), (w_codes, w_scales) = h1_q[n], w_q[g]
@@ -201,7 +219,8 @@ def tile_rdecommunicationlstm_pb_t_kernel(
             )
 
         def quantise_hidden(n):
-            h2_q[n] = quantise(h2[n], stage, "h2")
+            h2_q[n] = operand(stage, "h2")
+            quantise(h2[n], h2_q[n])
 
         def head_product(n, j):
             codes, scales = h2_q[n]
@@ -269,14 +288,11 @@ def tile_rdecommunicationlstm_pb_t_kernel(
                 out=out_1[n * ROWS : (n + 1) * ROWS, :].rearrange("(r j) c -> r j c", j=PACK), in_=v
             )
 
-        h1_grouped[0] = regroup(h1_raw[0], (copy_on_vector, copy_on_scalar))
-        h1_q[0] = quantise(h1_grouped[0], stage, "h1", pieces=2)
-        w_grouped[GATE_I] = regroup(w_raw[GATE_I], (copy_on_scalar, copy_on_scalar))
-        w_q[GATE_I] = quantise(w_grouped[GATE_I], consts, "w%d" % GATE_I, pieces=2)
+        h1_q[0] = prepare(h1_raw[0], (copy_on_vector, copy_on_scalar), stage, "h1")
+        w_q[GATE_I] = prepare(w_raw[GATE_I], (copy_on_scalar, copy_on_scalar), consts, "w%d" % GATE_I)
 
         def prepare_gate(g):
-            w_grouped[g] = regroup(w_raw[g], (copy_on_vector, copy_on_vector))
-            w_q[g] = quantise(w_grouped[g], consts, "w%d" % g)
+            w_q[g] = prepare(w_raw[g], (copy_on_vector, copy_on_vector), consts, "w%d" % g)
 
         gate(0, GATE_I, (0, 1))
         prepare_gate(GATE_G)
@@ -289,12 +305,15 @@ def tile_rdecommunicationlstm_pb_t_kernel(
 
         for n in range(NBLK):
             last = n - 1
-            on_tensor = OFF_VECTOR[:1] if n == 0 else OFF_VECTOR
-            on_vector_cells = [t for t in range(PACK) if t not in on_tensor]
+            on_tensor = OFF_VECTOR[:1] if n < 2 else OFF_VECTOR
+            on_gpsimd = PRODUCT_ON_GPSIMD if 1 < n < NBLK - 2 else PRODUCT_ON_GPSIMD[:2]
+            on_vector_cells = [t for t in reversed(range(PACK)) if t not in on_tensor]
             if n == 0:
                 prepare_gate(GATE_F)
             else:
                 gate(n, GATE_I)
+                if 1 < n < NBLK - 2:
+                    transpose_h1(n + 2)
                 hidden(last)
                 quantise_hidden(last)
                 if 1 < n < NBLK - 1:
@@ -303,7 +322,7 @@ def tile_rdecommunicationlstm_pb_t_kernel(
             if n == 0:
                 prepare_gate(GATE_O)
                 gate(n, GATE_F)
-                head_q = quantise(regroup(head_raw, (copy_on_vector, copy_on_vector)), consts, "head")
+                head_q = prepare(head_raw, (copy_on_vector, copy_on_vector), consts, "head")
             else:
                 head_product(last, 0)
                 head_product(last, 1)
@@ -318,16 +337,19 @@ def tile_rdecommunicationlstm_pb_t_kernel(
                 head_sum(last, 2)
                 head_sum(last, 3)
                 row_stats(last)
-            for t in OFF_VECTOR:
+            for t in on_gpsimd:
                 input_times_candidate(nc.gpsimd, n, slice(t, t + 1))
-            input_times_candidate(nc.vector, n, slice(len(OFF_VECTOR), PACK))
+            gate(n, GATE_O)
+            if 1 < n < NBLK - 2:
+                copy_h1(n + 2, copy_on_vector)
+            input_times_candidate(nc.vector, n, slice(len(on_gpsimd), PACK))
             for t in on_vector_cells:
                 new_cell(n, t)
-            gate(n, GATE_O)
             if n > 0:
                 sigmoid_spread(last)
             if n == 0:
-                regroup_h1(1, (copy_on_scalar, copy_on_scalar))
+                transpose_h1(1)
+                copy_h1(1, copy_on_scalar)
                 for half in range(2):
                     cols = slice(half * 2 * OUT, (half + 1) * 2 * OUT)
                     spread_ps = psum_gate.tile([P, 2 * OUT], F32, tag="gate")
@@ -335,7 +357,8 @@ def tile_rdecommunicationlstm_pb_t_kernel(
                     nc.vector.tensor_copy(out=spread[:, cols], in_=spread_ps[:])
                 quantise_h1(1)
             elif n == 1:
-                regroup_h1(2, (copy_on_vector, copy_on_vector))
+                transpose_h1(2)
+                copy_h1(2, copy_on_vector)
                 quantise_h1(2)
             for t in on_tensor:
                 open_cell(n, t)
@@ -347,8 +370,9 @@ def tile_rdecommunicationlstm_pb_t_kernel(
                 tanh_cell(n, t, cell_ps[n, t][:])
             if n > 1:
                 normalise(n - 2)
-            if 0 < n < NBLK - 2:
-                regroup_h1(n + 2, (copy_on_vector, copy_on_vector))
+            if n == 1:
+                transpose_h1(3)
+                copy_h1(3, copy_on_vector)
 
         last = NBLK - 1
         hidden(last)

@@ -26,7 +26,7 @@ SIG_MIN = 1e-6
 SIG_SCALE = math.exp(-SIG_MIN)
 SIG_FLOOR = 2.0**-62
 
-PRODUCT_ON_GPSIMD = (0, 1, 2)
+PRODUCT_ON_GPSIMD = (0, 1)
 OFF_VECTOR = (0, 1)
 
 FLOPS = 2 * BATCH * HID * (NG * HID) + 2 * BATCH * HID * (2 * OUT)
@@ -141,11 +141,14 @@ def tile_rdecommunicationlstm_pb_t_kernel(
                 in_=values[:, PACK * rows.start : PACK * rows.stop],
             )
 
+        def prepare_half(raw, grouped, codes_scales, half, copy_out):
+            copy_half(transpose_half(raw, half), grouped, half, copy_out)
+            quantise(grouped, codes_scales, slice(half * ROWS // 2, (half + 1) * ROWS // 2))
+
         def prepare(raw, copies, pool, name):
             grouped, codes_scales = grouped_tile(), operand(pool, name)
             for half, copy_out in enumerate(copies):
-                copy_half(transpose_half(raw, half), grouped, half, copy_out)
-                quantise(grouped, codes_scales, slice(half * ROWS // 2, (half + 1) * ROWS // 2))
+                prepare_half(raw, grouped, codes_scales, half, copy_out)
             return codes_scales
 
         copy_on_vector, copy_on_scalar = nc.vector.tensor_copy, nc.scalar.copy
@@ -155,9 +158,9 @@ def tile_rdecommunicationlstm_pb_t_kernel(
         def transpose_h1(n):
             h1_banks[n] = [transpose_half(h1_raw[n], half) for half in range(2)]
 
-        def copy_h1(n, copy_out):
+        def copy_h1(n, copies):
             h1_grouped[n] = grouped_tile()
-            for half in range(2):
+            for half, copy_out in enumerate(copies):
                 copy_half(h1_banks[n][half], h1_grouped[n], half, copy_out)
 
         def quantise_h1(n):
@@ -260,12 +263,14 @@ def tile_rdecommunicationlstm_pb_t_kernel(
                 out=sigs[n][:, tiles, :], in_=lin[:, n, 1, tiles, :], func=ACT.Sigmoid, bias=0.0, scale=-1.0
             )
 
-        def normalise(n):
-            for j in range(PACK):
+        def centre(n, tiles=range(PACK)):
+            for j in tiles:
                 nc.vector.scalar_tensor_tensor(
                     out=lin[:, n, 0, j, :], in0=lin[:, n, 0, j, :], scalar=stats[:, n, j // 2, j % 2, 1:2],
                     in1=ln_g_all, op0=ALU.subtract, op1=ALU.mult,
                 )
+
+        def scale(n):
             for j in range(PACK):
                 nc.vector.scalar_tensor_tensor(
                     out=lin[:, n, 0, j, :], in0=lin[:, n, 0, j, :], scalar=rstd[:, n, j : j + 1], in1=ln_b_all,
@@ -276,16 +281,12 @@ def tile_rdecommunicationlstm_pb_t_kernel(
                 in_=lin[:, n, 0, :, :],
             )
 
-        def softplus_log(n):
-            v = lin[:, n, 1, :, :]
-            nc.scalar.activation(
-                out=sigs[n][:], in_=sigs[n][:], func=ACT.Ln, bias=SIG_SCALE * SIG_FLOOR, scale=SIG_SCALE
-            )
-            nc.vector.scalar_tensor_tensor(
-                out=v, in0=sigs[n][:], scalar=-1.0, in1=v, op0=ALU.mult, op1=ALU.max,
-            )
+        def softplus_log(n, tiles=slice(0, PACK)):
+            v, sig = lin[:, n, 1, tiles, :], sigs[n][:, tiles, :]
+            nc.scalar.activation(out=sig, in_=sig, func=ACT.Ln, bias=SIG_SCALE * SIG_FLOOR, scale=SIG_SCALE)
+            nc.vector.scalar_tensor_tensor(out=v, in0=sig, scalar=-1.0, in1=v, op0=ALU.mult, op1=ALU.max)
             nc.sync.dma_start(
-                out=out_1[n * ROWS : (n + 1) * ROWS, :].rearrange("(r j) c -> r j c", j=PACK), in_=v
+                out=out_1[n * ROWS : (n + 1) * ROWS, :].rearrange("(r j) c -> r j c", j=PACK)[:, tiles, :], in_=v
             )
 
         h1_q[0] = prepare(h1_raw[0], (copy_on_vector, copy_on_scalar), stage, "h1")
@@ -294,8 +295,10 @@ def tile_rdecommunicationlstm_pb_t_kernel(
         def prepare_gate(g):
             w_q[g] = prepare(w_raw[g], (copy_on_vector, copy_on_vector), consts, "w%d" % g)
 
+        g_grouped, w_q[GATE_G] = grouped_tile(), operand(consts, "w%d" % GATE_G)
+        prepare_half(w_raw[GATE_G], g_grouped, w_q[GATE_G], 0, copy_on_vector)
         gate(0, GATE_I, (0, 1))
-        prepare_gate(GATE_G)
+        prepare_half(w_raw[GATE_G], g_grouped, w_q[GATE_G], 1, copy_on_vector)
         gate(0, GATE_I, (2, 3))
 
         spread = consts.tile([P, 4 * OUT], F32)
@@ -306,7 +309,7 @@ def tile_rdecommunicationlstm_pb_t_kernel(
         for n in range(NBLK):
             last = n - 1
             on_tensor = OFF_VECTOR[:1] if n < 2 else OFF_VECTOR
-            on_gpsimd = PRODUCT_ON_GPSIMD if 1 < n < NBLK - 2 else PRODUCT_ON_GPSIMD[:2]
+            on_gpsimd = PRODUCT_ON_GPSIMD
             on_vector_cells = [t for t in reversed(range(PACK)) if t not in on_tensor]
             if n == 0:
                 prepare_gate(GATE_F)
@@ -318,6 +321,8 @@ def tile_rdecommunicationlstm_pb_t_kernel(
                 quantise_hidden(last)
                 if 1 < n < NBLK - 1:
                     quantise_h1(n + 1)
+                elif n > 1:
+                    centre(n - 2, (0, 1))
             gate(n, GATE_G)
             if n == 0:
                 prepare_gate(GATE_O)
@@ -328,12 +333,12 @@ def tile_rdecommunicationlstm_pb_t_kernel(
                 head_product(last, 1)
                 if n > 1:
                     row_rstd(n - 2)
-                gate(n, GATE_F, (0, 1))
+                gate(n, GATE_F, (0, 1, 2))
                 head_sum(last, 0)
                 head_product(last, 2)
+                gate(n, GATE_F, (3,))
                 head_sum(last, 1)
                 head_product(last, 3)
-                gate(n, GATE_F, (2, 3))
                 head_sum(last, 2)
                 head_sum(last, 3)
                 row_stats(last)
@@ -341,7 +346,7 @@ def tile_rdecommunicationlstm_pb_t_kernel(
                 input_times_candidate(nc.gpsimd, n, slice(t, t + 1))
             gate(n, GATE_O)
             if 1 < n < NBLK - 2:
-                copy_h1(n + 2, copy_on_vector)
+                copy_h1(n + 2, (copy_on_scalar, copy_on_vector))
             input_times_candidate(nc.vector, n, slice(len(on_gpsimd), PACK))
             for t in on_vector_cells:
                 new_cell(n, t)
@@ -349,16 +354,16 @@ def tile_rdecommunicationlstm_pb_t_kernel(
                 sigmoid_spread(last)
             if n == 0:
                 transpose_h1(1)
-                copy_h1(1, copy_on_scalar)
+                copy_h1(1, (copy_on_scalar, copy_on_scalar))
+                quantise_h1(1)
                 for half in range(2):
                     cols = slice(half * 2 * OUT, (half + 1) * 2 * OUT)
                     spread_ps = psum_gate.tile([P, 2 * OUT], F32, tag="gate")
                     nc.tensor.matmul(out=spread_ps[:], lhsT=ones[:], rhs=head_rows[:, cols], start=True, stop=True)
                     nc.vector.tensor_copy(out=spread[:, cols], in_=spread_ps[:])
-                quantise_h1(1)
             elif n == 1:
                 transpose_h1(2)
-                copy_h1(2, copy_on_vector)
+                copy_h1(2, (copy_on_vector, copy_on_vector))
                 quantise_h1(2)
             for t in on_tensor:
                 open_cell(n, t)
@@ -369,14 +374,16 @@ def tile_rdecommunicationlstm_pb_t_kernel(
             for t in on_tensor:
                 tanh_cell(n, t, cell_ps[n, t][:])
             if n > 1:
-                normalise(n - 2)
+                centre(n - 2, range(PACK) if n < NBLK - 1 else (2, 3))
+                scale(n - 2)
             if n == 1:
                 transpose_h1(3)
-                copy_h1(3, copy_on_vector)
+                copy_h1(3, (copy_on_vector, copy_on_vector))
 
         last = NBLK - 1
         hidden(last)
         quantise_hidden(last)
+        centre(last - 1)
         row_rstd(last - 1)
         for j in range(PACK):
             head_product(last, j)
@@ -384,8 +391,11 @@ def tile_rdecommunicationlstm_pb_t_kernel(
             sigmoid_spread(last, slice(j, j + 1))
         row_stats(last)
         row_rstd(last)
-        normalise(last - 1)
-        for n in range(NBLK):
+        scale(last - 1)
+        centre(last)
+        softplus_log(0)
+        scale(last)
+        for n in range(1, last):
             softplus_log(n)
-            if n == 0:
-                normalise(last)
+        for half in range(2):
+            softplus_log(last, slice(2 * half, 2 * half + 2))

@@ -79,7 +79,7 @@ def tile_rdecommunicationlstm_pb_t_kernel(
         nc.sync.dma_start(out=head_raw_tiles[:, 0:2, :], in_=mu_W.rearrange("(a r) k -> r a k", a=2))
         nc.sync.dma_start(out=head_raw_tiles[:, 2:4, :], in_=sig_W.rearrange("(a r) k -> r a k", a=2))
         head_rows = consts.tile([P, 4 * OUT], BF16)
-        nc.gpsimd.memset(head_rows[:], 0.0)
+        nc.vector.memset(head_rows[:], 0.0)
         for slot, vector in enumerate((mu_b, sig_b, ln_g, ln_b)):
             nc.sync.dma_start(out=head_rows[0:1, slot * OUT : (slot + 1) * OUT], in_=vector.unsqueeze(0))
         for n in range(2, NBLK):
@@ -109,6 +109,7 @@ def tile_rdecommunicationlstm_pb_t_kernel(
         lin = consts.tile([P, NBLK, 2, PACK, OUT], F32)
         stats = consts.tile([P, NBLK, 2, 2, 3], F32)
         var_eps = consts.tile([P, NBLK, PACK], F32)
+        var_released = consts.tile([P, NBLK, PACK], F32)
         rstd = consts.tile([P, NBLK, PACK], F32)
 
         def grouped_tile():
@@ -249,12 +250,15 @@ def tile_rdecommunicationlstm_pb_t_kernel(
                     in_=lin[:, n, 0, 2 * h : 2 * h + 2, :].rearrange("r e c -> r c e"),
                 )
 
-        def row_rstd(n):
+        def row_var(n):
             nc.vector.tensor_scalar(
                 out=var_eps[:, n, :], in0=stats[:, n, :, :, 2].rearrange("r h e -> r (h e)"),
                 scalar1=1.0 / OUT, scalar2=LN_EPS, op0=ALU.mult, op1=ALU.add,
             )
-            nc.gpsimd.tensor_tensor(out=rstd[:, n, :], in0=var_eps[:, n, :], in1=minus_half[:], op=ALU.pow)
+            nc.gpsimd.tensor_copy(out=var_released[:, n, :], in_=var_eps[:, n, :])
+
+        def row_rstd(n):
+            nc.gpsimd.tensor_tensor(out=rstd[:, n, :], in0=var_released[:, n, :], in1=minus_half[:], op=ALU.pow)
 
         def sigmoid_spread(n, tiles=slice(0, PACK)):
             if n not in sigs:
@@ -270,12 +274,14 @@ def tile_rdecommunicationlstm_pb_t_kernel(
                     in1=ln_g_all, op0=ALU.subtract, op1=ALU.mult,
                 )
 
-        def scale(n):
-            for j in range(PACK):
+        def scale(n, tiles=range(PACK)):
+            for j in tiles:
                 nc.vector.scalar_tensor_tensor(
                     out=lin[:, n, 0, j, :], in0=lin[:, n, 0, j, :], scalar=rstd[:, n, j : j + 1], in1=ln_b_all,
                     op0=ALU.mult, op1=ALU.add,
                 )
+
+        def store_mu(n):
             nc.sync.dma_start(
                 out=out_0[n * ROWS : (n + 1) * ROWS, :].rearrange("(r j) c -> r j c", j=PACK),
                 in_=lin[:, n, 0, :, :],
@@ -315,13 +321,20 @@ def tile_rdecommunicationlstm_pb_t_kernel(
                 prepare_gate(GATE_F)
             else:
                 gate(n, GATE_I)
-                if 1 < n < NBLK - 2:
+                if n == 1:
+                    transpose_h1(2)
+                elif n < NBLK - 2:
                     transpose_h1(n + 2)
                 hidden(last)
+                if n > 2:
+                    scale(n - 3, (3,))
+                    store_mu(n - 3)
                 quantise_hidden(last)
-                if 1 < n < NBLK - 1:
+                if n == 1:
+                    copy_h1(2, (copy_on_vector, copy_on_vector))
+                elif n < NBLK - 1:
                     quantise_h1(n + 1)
-                elif n > 1:
+                else:
                     centre(n - 2, (0, 1))
             gate(n, GATE_G)
             if n == 0:
@@ -329,11 +342,12 @@ def tile_rdecommunicationlstm_pb_t_kernel(
                 gate(n, GATE_F)
                 head_q = prepare(head_raw, (copy_on_vector, copy_on_vector), consts, "head")
             else:
+                gate(n, GATE_F, (0,))
                 head_product(last, 0)
                 head_product(last, 1)
                 if n > 1:
-                    row_rstd(n - 2)
-                gate(n, GATE_F, (0, 1, 2))
+                    row_var(n - 2)
+                gate(n, GATE_F, (1, 2))
                 head_sum(last, 0)
                 head_product(last, 2)
                 gate(n, GATE_F, (3,))
@@ -344,10 +358,14 @@ def tile_rdecommunicationlstm_pb_t_kernel(
                 row_stats(last)
             for t in on_gpsimd:
                 input_times_candidate(nc.gpsimd, n, slice(t, t + 1))
+            if n > 1:
+                row_rstd(n - 2)
             gate(n, GATE_O)
             if 1 < n < NBLK - 2:
                 copy_h1(n + 2, (copy_on_scalar, copy_on_vector))
             input_times_candidate(nc.vector, n, slice(len(on_gpsimd), PACK))
+            if n > 1:
+                centre(n - 2, (2,))
             for t in on_vector_cells:
                 new_cell(n, t)
             if n > 0:
@@ -361,12 +379,10 @@ def tile_rdecommunicationlstm_pb_t_kernel(
                     spread_ps = psum_gate.tile([P, 2 * OUT], F32, tag="gate")
                     nc.tensor.matmul(out=spread_ps[:], lhsT=ones[:], rhs=head_rows[:, cols], start=True, stop=True)
                     nc.vector.tensor_copy(out=spread[:, cols], in_=spread_ps[:])
-            elif n == 1:
-                transpose_h1(2)
-                copy_h1(2, (copy_on_vector, copy_on_vector))
-                quantise_h1(2)
             for t in on_tensor:
                 open_cell(n, t)
+            if n == 1:
+                transpose_h1(3)
             for t in on_tensor:
                 close_cell(n, t)
             for t in on_vector_cells:
@@ -374,27 +390,34 @@ def tile_rdecommunicationlstm_pb_t_kernel(
             for t in on_tensor:
                 tanh_cell(n, t, cell_ps[n, t][:])
             if n > 1:
-                centre(n - 2, range(PACK) if n < NBLK - 1 else (2, 3))
-                scale(n - 2)
+                centre(n - 2, (0, 1, 3) if n < NBLK - 1 else (3,))
+                scale(n - 2, (0, 1, 2))
             if n == 1:
-                transpose_h1(3)
+                quantise_h1(2)
                 copy_h1(3, (copy_on_vector, copy_on_vector))
 
         last = NBLK - 1
+        centre(last - 1, (0, 1))
         hidden(last)
+        scale(last - 2, (3,))
+        store_mu(last - 2)
         quantise_hidden(last)
-        centre(last - 1)
+        centre(last - 1, (2, 3))
+        row_var(last - 1)
         row_rstd(last - 1)
         for j in range(PACK):
             head_product(last, j)
             head_sum(last, j)
             sigmoid_spread(last, slice(j, j + 1))
         row_stats(last)
+        row_var(last)
         row_rstd(last)
         scale(last - 1)
+        store_mu(last - 1)
         centre(last)
         softplus_log(0)
         scale(last)
+        store_mu(last)
         for n in range(1, last):
             softplus_log(n)
         for half in range(2):

@@ -26,8 +26,8 @@ SIG_MIN = 1e-6
 SIG_SCALE = math.exp(-SIG_MIN)
 SIG_FLOOR = 2.0**-62
 
-PRODUCT_ON_GPSIMD = (0, 1)
 OFF_VECTOR = (0, 1)
+ON_GPSIMD_FIRST = (0, 1, 2)
 
 FLOPS = 2 * BATCH * HID * (NG * HID) + 2 * BATCH * HID * (2 * OUT)
 
@@ -58,15 +58,12 @@ def tile_rdecommunicationlstm_pb_t_kernel(
         def h1_rows(n):
             return h1[n * ROWS : (n + 1) * ROWS, :].rearrange("(r j) k -> r (j k)", j=PACK)
 
-        bias_parts = []
-        for vector in (hh_gates, b_ih1, b_hh1):
-            part = consts.tile([P, NG, PACK], BF16, name="bias_part%d" % len(bias_parts))
-            nc.scalar.dma_start(out=part[:], in_=vector.rearrange("(g m t) -> m g t", g=NG, t=PACK))
-            bias_parts.append(part)
-        c_init_bf = consts.tile([P, PACK], BF16)
-        nc.scalar.dma_start(out=c_init_bf[:], in_=c_init.rearrange("(m t) -> m t", t=PACK))
-
         h1_raw = {0: load_rows(h1_rows(0), pieces=2)}
+        unit_rows = consts.tile([P, HID], BF16)
+        nc.vector.memset(unit_rows[:], 0.0)
+        for v, vector in enumerate((hh_gates, b_ih1, b_hh1)):
+            nc.sync.dma_start(out=unit_rows[32 * v : 32 * v + NG, :], in_=vector.rearrange("(g k) -> g k", g=NG))
+        nc.sync.dma_start(out=unit_rows[96:97, :], in_=c_init.unsqueeze(0))
         w_raw = {}
         for g in GATE_ORDER:
             w_raw[g] = load_rows(
@@ -94,17 +91,31 @@ def tile_rdecommunicationlstm_pb_t_kernel(
         nc.vector.memset(ones[:], 1.0)
         minus_half = consts.tile([P, PACK], F32)
         nc.vector.memset(minus_half[:], -0.5)
-        gate_bias = consts.tile([P, NG, PACK], F32)
-        nc.gpsimd.tensor_tensor(out=gate_bias[:], in0=bias_parts[1][:], in1=bias_parts[2][:], op=ALU.add)
-        nc.gpsimd.tensor_tensor(out=gate_bias[:], in0=gate_bias[:], in1=bias_parts[0][:], op=ALU.add)
-        c_init_f = consts.tile([P, PACK], F32)
-        nc.gpsimd.tensor_copy(out=c_init_f[:], in_=c_init_bf[:])
+        pick = consts.tile([P, NG + 1], BF16)
+        two = consts.tile([P, NG], F32)
+        nc.gpsimd.tensor_tensor(out=two[:], in0=identity[:, 0:NG], in1=identity[:, 32 : 32 + NG], op=ALU.add)
+        nc.gpsimd.tensor_tensor(out=pick[:, 0:NG], in0=two[:], in1=identity[:, 64 : 64 + NG], op=ALU.add)
+        nc.gpsimd.tensor_copy(out=pick[:, NG : NG + 1], in_=identity[:, 96:97])
+        per_unit = consts.tile([P, PACK, NG + 1], F32)
+
+        def spread_units():
+            units_ps = psum_head.tile([P, PACK, NG + 1], F32, name="head")
+            for t in range(PACK):
+                nc.tensor.matmul(
+                    out=units_ps[:, t, :], lhsT=unit_rows[:].rearrange("v (m t) -> v t m", t=PACK)[:, t, :], rhs=pick[:],
+                    start=True, stop=True,
+                )
+            nc.vector.tensor_copy(out=per_unit[:], in_=units_ps[:])
+
+        def make_diagonals():
+            for t in OFF_VECTOR:
+                nc.gpsimd.tensor_scalar(
+                    out=diag_c[t][:], in0=identity[:], scalar1=per_unit[:, t, NG : NG + 1], scalar2=None, op0=ALU.mult
+                )
+
         diag_c = {}
         for t in OFF_VECTOR:
             diag_c[t] = consts.tile([P, P], F32, name="diag_c%d" % t)
-            nc.gpsimd.tensor_scalar(
-                out=diag_c[t][:], in0=identity[:], scalar1=c_init_f[:, t : t + 1], scalar2=None, op0=ALU.mult
-            )
 
         lin = consts.tile([P, NBLK, 2, PACK, OUT], F32)
         stats = consts.tile([P, NBLK, 2, 2, 3], F32)
@@ -184,7 +195,7 @@ def tile_rdecommunicationlstm_pb_t_kernel(
                 nc.scalar.activation(
                     out=act[n, g][:, t, :], in_=gate_ps[:],
                     func=ACT.Tanh if g == GATE_G else ACT.Sigmoid,
-                    bias=gate_bias[:, g, t : t + 1], scale=1.0,
+                    bias=per_unit[:, t, g : g + 1], scale=1.0,
                 )
 
         def input_times_candidate(engine, n, tiles):
@@ -206,7 +217,7 @@ def tile_rdecommunicationlstm_pb_t_kernel(
 
         def new_cell(n, t):
             nc.vector.scalar_tensor_tensor(
-                out=act[n, GATE_F][:, t, :], in0=act[n, GATE_F][:, t, :], scalar=c_init_f[:, t : t + 1],
+                out=act[n, GATE_F][:, t, :], in0=act[n, GATE_F][:, t, :], scalar=per_unit[:, t, NG : NG + 1],
                 in1=act[n, GATE_I][:, t, :], op0=ALU.mult, op1=ALU.add,
             )
 
@@ -296,7 +307,9 @@ def tile_rdecommunicationlstm_pb_t_kernel(
             )
 
         h1_q[0] = prepare(h1_raw[0], (copy_on_vector, copy_on_scalar), stage, "h1")
+        spread_units()
         w_q[GATE_I] = prepare(w_raw[GATE_I], (copy_on_scalar, copy_on_scalar), consts, "w%d" % GATE_I)
+        make_diagonals()
 
         def prepare_gate(g):
             w_q[g] = prepare(w_raw[g], (copy_on_vector, copy_on_vector), consts, "w%d" % g)
@@ -307,94 +320,105 @@ def tile_rdecommunicationlstm_pb_t_kernel(
         prepare_half(w_raw[GATE_G], g_grouped, w_q[GATE_G], 1, copy_on_vector)
         gate(0, GATE_I, (2, 3))
 
+        def cell(n, on_tensor, between=None):
+            on_vector = [t for t in reversed(range(PACK)) if t not in on_tensor]
+            for t in on_vector:
+                new_cell(n, t)
+            for t in on_tensor:
+                open_cell(n, t)
+            if between:
+                between()
+            for t in on_tensor:
+                close_cell(n, t)
+            for t in on_vector:
+                tanh_cell(n, t, act[n, GATE_F][:, t, :])
+            for t in on_tensor:
+                tanh_cell(n, t, cell_ps[n, t][:])
+
         spread = consts.tile([P, 4 * OUT], F32)
         head_bias = spread[:, 0 : 2 * OUT].rearrange("r (h c) -> r h c", h=2)
         ln_g_all = spread[:, 2 * OUT : 3 * OUT]
         ln_b_all = spread[:, 3 * OUT : 4 * OUT]
 
-        for n in range(NBLK):
+        def repeat_heads(half):
+            bank = psum_head.tile([P, 2 * OUT], F32, name="head")
+            cols = slice(half * 2 * OUT, (half + 1) * 2 * OUT)
+            nc.tensor.matmul(out=bank[:], lhsT=ones[:], rhs=head_rows[:, cols], start=True, stop=True)
+            return bank
+
+        def spread_heads(half, bank):
+            nc.vector.tensor_copy(out=spread[:, half * 2 * OUT : (half + 1) * 2 * OUT], in_=bank[:])
+
+        prepare_gate(GATE_F)
+        gate(0, GATE_G)
+        prepare_gate(GATE_O)
+        gate(0, GATE_F)
+        transpose_h1(1)
+        for t in ON_GPSIMD_FIRST:
+            input_times_candidate(nc.gpsimd, 0, slice(t, t + 1))
+        gate(0, GATE_O)
+        input_times_candidate(nc.vector, 0, slice(len(ON_GPSIMD_FIRST), PACK))
+        copy_h1(1, (copy_on_vector, copy_on_vector))
+        head_banks = []
+        cell(0, OFF_VECTOR[:1], lambda: head_banks.extend([transpose_half(head_raw, half) for half in range(2)]))
+        quantise_h1(1)
+        head_grouped, head_q = grouped_tile(), operand(consts, "head")
+        for half in range(2):
+            copy_half(head_banks[half], head_grouped, half, copy_on_vector)
+        quantise(head_grouped, head_q)
+        spread_heads(0, repeat_heads(0))
+
+        for n in range(1, NBLK):
             last = n - 1
-            on_tensor = OFF_VECTOR[:1] if n < 2 else OFF_VECTOR
-            on_gpsimd = PRODUCT_ON_GPSIMD
-            on_vector_cells = [t for t in reversed(range(PACK)) if t not in on_tensor]
-            if n == 0:
-                prepare_gate(GATE_F)
+            gate(n, GATE_I)
+            if n < NBLK - 2:
+                transpose_h1(n + 1 if n == 1 else n + 2)
+            hidden(last)
+            if n > 2:
+                scale(n - 3, (3,))
+                store_mu(n - 3)
+            quantise_hidden(last)
+            if n == 1:
+                copy_h1(2, (copy_on_vector, copy_on_vector))
+            elif n < NBLK - 1:
+                quantise_h1(n + 1)
             else:
-                gate(n, GATE_I)
-                if n == 1:
-                    transpose_h1(2)
-                elif n < NBLK - 2:
-                    transpose_h1(n + 2)
-                hidden(last)
-                if n > 2:
-                    scale(n - 3, (3,))
-                    store_mu(n - 3)
-                quantise_hidden(last)
-                if n == 1:
-                    copy_h1(2, (copy_on_vector, copy_on_vector))
-                elif n < NBLK - 1:
-                    quantise_h1(n + 1)
-                else:
-                    centre(n - 2, (0, 1))
+                centre(n - 2, (0, 1))
             gate(n, GATE_G)
-            if n == 0:
-                prepare_gate(GATE_O)
-                gate(n, GATE_F)
-                head_q = prepare(head_raw, (copy_on_vector, copy_on_vector), consts, "head")
-            else:
-                gate(n, GATE_F, (0,))
-                head_product(last, 0)
-                head_product(last, 1)
-                if n > 1:
-                    row_var(n - 2)
-                gate(n, GATE_F, (1, 2))
-                head_sum(last, 0)
-                head_product(last, 2)
-                gate(n, GATE_F, (3,))
-                head_sum(last, 1)
-                head_product(last, 3)
-                head_sum(last, 2)
-                head_sum(last, 3)
-                row_stats(last)
-            for t in on_gpsimd:
+            gate(n, GATE_F, (0,))
+            head_product(last, 0)
+            head_product(last, 1)
+            if n > 1:
+                row_var(n - 2)
+            gate(n, GATE_F, (1, 2))
+            head_sum(last, 0)
+            head_product(last, 2)
+            gate(n, GATE_F, (3,))
+            head_sum(last, 1)
+            head_product(last, 3)
+            head_sum(last, 2)
+            head_sum(last, 3)
+            row_stats(last)
+            for t in OFF_VECTOR:
                 input_times_candidate(nc.gpsimd, n, slice(t, t + 1))
             if n > 1:
                 row_rstd(n - 2)
             gate(n, GATE_O)
             if 1 < n < NBLK - 2:
                 copy_h1(n + 2, (copy_on_scalar, copy_on_vector))
-            input_times_candidate(nc.vector, n, slice(len(on_gpsimd), PACK))
+            input_times_candidate(nc.vector, n, slice(len(OFF_VECTOR), PACK))
             if n > 1:
                 centre(n - 2, (2,))
-            for t in on_vector_cells:
-                new_cell(n, t)
-            if n > 0:
-                sigmoid_spread(last)
-            if n == 0:
-                transpose_h1(1)
-                copy_h1(1, (copy_on_scalar, copy_on_scalar))
-                quantise_h1(1)
-                for half in range(2):
-                    cols = slice(half * 2 * OUT, (half + 1) * 2 * OUT)
-                    spread_ps = psum_gate.tile([P, 2 * OUT], F32, tag="gate")
-                    nc.tensor.matmul(out=spread_ps[:], lhsT=ones[:], rhs=head_rows[:, cols], start=True, stop=True)
-                    nc.vector.tensor_copy(out=spread[:, cols], in_=spread_ps[:])
-            for t in on_tensor:
-                open_cell(n, t)
+            sigmoid_spread(last)
             if n == 1:
-                transpose_h1(3)
-            for t in on_tensor:
-                close_cell(n, t)
-            for t in on_vector_cells:
-                tanh_cell(n, t, act[n, GATE_F][:, t, :])
-            for t in on_tensor:
-                tanh_cell(n, t, cell_ps[n, t][:])
-            if n > 1:
-                centre(n - 2, (0, 1, 3) if n < NBLK - 1 else (3,))
-                scale(n - 2, (0, 1, 2))
-            if n == 1:
+                cell(n, OFF_VECTOR[:1], lambda: transpose_h1(3))
                 quantise_h1(2)
                 copy_h1(3, (copy_on_vector, copy_on_vector))
+                spread_heads(1, repeat_heads(1))
+            else:
+                cell(n, OFF_VECTOR)
+                centre(n - 2, (0, 1, 3) if n < NBLK - 1 else (3,))
+                scale(n - 2, (0, 1, 2))
 
         last = NBLK - 1
         centre(last - 1, (0, 1))

@@ -47,6 +47,9 @@ def tile_rdecommunicationlstm_pb_t_kernel(
         psum_head = pools.enter_context(tc.psum_pool(name="psum_head", bufs=2))
         pools.enter_context(tc.manual_schedule())
 
+        zeros = consts.tile([P, K], BF16)
+        nc.vector.memset(zeros[:], 0.0)
+
         def load_rows(source, pieces=1):
             raw = raw_pool.tile([P, PACK * K], BF16, name="raw")
             width = PACK * K // pieces
@@ -89,7 +92,7 @@ def tile_rdecommunicationlstm_pb_t_kernel(
         make_identity(nc, identity[:])
         ones = consts.tile([P, P], BF16)
         nc.vector.memset(ones[:], 1.0)
-        minus_half = consts.tile([P, PACK], F32)
+        minus_half = consts.tile([P, 2, 2], F32)
         nc.vector.memset(minus_half[:], -0.5)
         pick = consts.tile([P, NG + 1], BF16)
         two = consts.tile([P, NG], F32)
@@ -119,9 +122,9 @@ def tile_rdecommunicationlstm_pb_t_kernel(
 
         lin = consts.tile([P, NBLK, 2, PACK, OUT], F32)
         stats = consts.tile([P, NBLK, 2, 2, 3], F32)
-        var_eps = consts.tile([P, NBLK, PACK], F32)
-        var_released = consts.tile([P, NBLK, PACK], F32)
-        rstd = consts.tile([P, NBLK, PACK], F32)
+        var_eps = consts.tile([P, NBLK, 2, 2], F32)
+        var_released = consts.tile([P, NBLK, 2, 2], F32)
+        rstd = consts.tile([P, NBLK, 2, 2], F32)
 
         def grouped_tile():
             return stage.tile([P, ROWS * PACK], BF16, name="grouped", align_bytes=64)
@@ -254,22 +257,24 @@ def tile_rdecommunicationlstm_pb_t_kernel(
                 op=ALU.add,
             )
 
-        def row_stats(n):
-            for h in range(2):
+        def row_stats(n, pairs=(0, 1)):
+            for h in pairs:
                 nc.vector.bn_stats(
                     out=stats[:, n, h, :, :].rearrange("r e s -> r (e s)"),
                     in_=lin[:, n, 0, 2 * h : 2 * h + 2, :].rearrange("r e c -> r c e"),
                 )
 
-        def row_var(n):
+        def row_var(n, pairs=slice(0, 2)):
             nc.vector.tensor_scalar(
-                out=var_eps[:, n, :], in0=stats[:, n, :, :, 2].rearrange("r h e -> r (h e)"),
+                out=var_eps[:, n, pairs, :], in0=stats[:, n, pairs, :, 2],
                 scalar1=1.0 / OUT, scalar2=LN_EPS, op0=ALU.mult, op1=ALU.add,
             )
-            nc.gpsimd.tensor_copy(out=var_released[:, n, :], in_=var_eps[:, n, :])
+            nc.gpsimd.tensor_copy(out=var_released[:, n, pairs, :], in_=var_eps[:, n, pairs, :])
 
-        def row_rstd(n):
-            nc.gpsimd.tensor_tensor(out=rstd[:, n, :], in0=var_released[:, n, :], in1=minus_half[:], op=ALU.pow)
+        def row_rstd(n, pairs=slice(0, 2)):
+            nc.gpsimd.tensor_tensor(
+                out=rstd[:, n, pairs, :], in0=var_released[:, n, pairs, :], in1=minus_half[:, pairs, :], op=ALU.pow
+            )
 
         def sigmoid_spread(n, tiles=slice(0, PACK)):
             if n not in sigs:
@@ -288,7 +293,7 @@ def tile_rdecommunicationlstm_pb_t_kernel(
         def scale(n, tiles=range(PACK)):
             for j in tiles:
                 nc.vector.scalar_tensor_tensor(
-                    out=lin[:, n, 0, j, :], in0=lin[:, n, 0, j, :], scalar=rstd[:, n, j : j + 1], in1=ln_b_all,
+                    out=lin[:, n, 0, j, :], in0=lin[:, n, 0, j, :], scalar=rstd[:, n, j // 2, j % 2 : j % 2 + 1], in1=ln_b_all,
                     op0=ALU.mult, op1=ALU.add,
                 )
 
@@ -306,9 +311,17 @@ def tile_rdecommunicationlstm_pb_t_kernel(
                 out=out_1[n * ROWS : (n + 1) * ROWS, :].rearrange("(r j) c -> r j c", j=PACK)[:, tiles, :], in_=v
             )
 
+        def keep_tensor_busy(products):
+            for product in range(products):
+                idle_ps = psum_gate.tile([P, ROWS], F32, tag="gate")
+                nc.tensor.matmul(out=idle_ps[:], lhsT=zeros[:, 0:P], rhs=zeros[:], start=True, stop=True)
+
+        keep_tensor_busy(3)
         h1_q[0] = prepare(h1_raw[0], (copy_on_vector, copy_on_scalar), stage, "h1")
+        keep_tensor_busy(1)
         spread_units()
         w_q[GATE_I] = prepare(w_raw[GATE_I], (copy_on_scalar, copy_on_scalar), consts, "w%d" % GATE_I)
+        keep_tensor_busy(1)
         make_diagonals()
 
         def prepare_gate(g):
@@ -399,14 +412,15 @@ def tile_rdecommunicationlstm_pb_t_kernel(
             head_sum(last, 2)
             head_sum(last, 3)
             row_stats(last)
-            for t in OFF_VECTOR:
+            on_gpsimd = ON_GPSIMD_FIRST if n == 1 else OFF_VECTOR
+            for t in on_gpsimd:
                 input_times_candidate(nc.gpsimd, n, slice(t, t + 1))
             if n > 1:
                 row_rstd(n - 2)
             gate(n, GATE_O)
             if 1 < n < NBLK - 2:
                 copy_h1(n + 2, (copy_on_scalar, copy_on_vector))
-            input_times_candidate(nc.vector, n, slice(len(OFF_VECTOR), PACK))
+            input_times_candidate(nc.vector, n, slice(len(on_gpsimd), PACK))
             if n > 1:
                 centre(n - 2, (2,))
             sigmoid_spread(last)
@@ -433,9 +447,11 @@ def tile_rdecommunicationlstm_pb_t_kernel(
             head_product(last, j)
             head_sum(last, j)
             sigmoid_spread(last, slice(j, j + 1))
-        row_stats(last)
-        row_var(last)
-        row_rstd(last)
+            if j % 2 == 1:
+                pair = slice(j // 2, j // 2 + 1)
+                row_stats(last, (j // 2,))
+                row_var(last, pair)
+                row_rstd(last, pair)
         scale(last - 1)
         store_mu(last - 1)
         centre(last)

@@ -129,9 +129,9 @@ def tile_rdecommunicationlstm_pb_t_kernel(
         def grouped_tile():
             return stage.tile([P, ROWS * PACK], BF16, name="grouped", align_bytes=64)
 
-        def transpose_half(raw, half):
+        def transpose_half(raw, half, pool=psum_t, tag="transposed"):
             words = raw[:].bitcast(F32).rearrange("r (a q u) -> r a u q", a=PACK, u=2)
-            bank = psum_t.tile([P, 2, 2, P], F32, tag="transposed")
+            bank = pool.tile([P, 2, 2, P], F32, tag=tag)
             for a in range(2):
                 for u in range(2):
                     nc.tensor.transpose(bank[:, a, u, :], words[:, 2 * half + a, u, :], identity[:])
@@ -156,14 +156,14 @@ def tile_rdecommunicationlstm_pb_t_kernel(
                 in_=values[:, PACK * rows.start : PACK * rows.stop],
             )
 
-        def prepare_half(raw, grouped, codes_scales, half, copy_out):
-            copy_half(transpose_half(raw, half), grouped, half, copy_out)
+        def prepare_half(raw, grouped, codes_scales, half, copy_out, *bank):
+            copy_half(transpose_half(raw, half, *bank), grouped, half, copy_out)
             quantise(grouped, codes_scales, slice(half * ROWS // 2, (half + 1) * ROWS // 2))
 
-        def prepare(raw, copies, pool, name):
+        def prepare(raw, copies, pool, name, *bank):
             grouped, codes_scales = grouped_tile(), operand(pool, name)
             for half, copy_out in enumerate(copies):
-                prepare_half(raw, grouped, codes_scales, half, copy_out)
+                prepare_half(raw, grouped, codes_scales, half, copy_out, *bank)
             return codes_scales
 
         copy_on_vector, copy_on_scalar = nc.vector.tensor_copy, nc.scalar.copy
@@ -320,8 +320,9 @@ def tile_rdecommunicationlstm_pb_t_kernel(
         h1_q[0] = prepare(h1_raw[0], (copy_on_vector, copy_on_scalar), stage, "h1")
         keep_tensor_busy(1)
         spread_units()
-        w_q[GATE_I] = prepare(w_raw[GATE_I], (copy_on_scalar, copy_on_scalar), consts, "w%d" % GATE_I)
-        keep_tensor_busy(1)
+        w_q[GATE_I] = prepare(
+            w_raw[GATE_I], (copy_on_scalar, copy_on_scalar), consts, "w%d" % GATE_I, psum_gate, "gate"
+        )
         make_diagonals()
 
         def prepare_gate(g):
@@ -381,6 +382,7 @@ def tile_rdecommunicationlstm_pb_t_kernel(
         quantise(head_grouped, head_q)
         spread_heads(0, repeat_heads(0))
 
+        spread_done = 0
         for n in range(1, NBLK):
             last = n - 1
             gate(n, GATE_I)
@@ -418,16 +420,19 @@ def tile_rdecommunicationlstm_pb_t_kernel(
             if n > 1:
                 row_rstd(n - 2)
             gate(n, GATE_O)
-            if 1 < n < NBLK - 2:
-                copy_h1(n + 2, (copy_on_scalar, copy_on_vector))
+            if n == 1:
+                transpose_h1(3)
+            if n < NBLK - 2:
+                copy_h1(n + 2, (copy_on_scalar, copy_on_scalar))
             input_times_candidate(nc.vector, n, slice(len(on_gpsimd), PACK))
             if n > 1:
                 centre(n - 2, (2,))
-            sigmoid_spread(last)
+            if n >= NBLK - 2:
+                sigmoid_spread(spread_done)
+                spread_done += 1
             if n == 1:
-                cell(n, OFF_VECTOR[:1], lambda: transpose_h1(3))
+                cell(n, OFF_VECTOR[:1])
                 quantise_h1(2)
-                copy_h1(3, (copy_on_vector, copy_on_vector))
                 spread_heads(1, repeat_heads(1))
             else:
                 cell(n, OFF_VECTOR)
@@ -443,6 +448,8 @@ def tile_rdecommunicationlstm_pb_t_kernel(
         centre(last - 1, (2, 3))
         row_var(last - 1)
         row_rstd(last - 1)
+        for n in range(spread_done, last):
+            sigmoid_spread(n)
         for j in range(PACK):
             head_product(last, j)
             head_sum(last, j)

import math
from contextlib import ExitStack

import concourse.mybir as mybir
from concourse.masks import make_identity

F32 = mybir.dt.float32
BF16 = mybir.dt.bfloat16
U32 = mybir.dt.uint32
U8 = mybir.dt.uint8
FP8X4 = mybir.dt.float8_e4m3fn_x4
ACT = mybir.ActivationFunctionType
ALU = mybir.AluOpType

P = 128
PACK = 4
K = P * PACK

BATCH, HID, OUT, NG = 4096, 512, 256, 4
ROWS = 512
NBLK = BATCH // ROWS
GATE_I, GATE_F, GATE_G, GATE_O = 0, 1, 2, 3
GATE_ORDER = (GATE_I, GATE_G, GATE_F, GATE_O)
LN_EPS = 1e-5
SIG_MIN = 1e-6
SIG_SCALE = math.exp(-SIG_MIN)
SIG_FLOOR = 2.0**-62

OFF_VECTOR = (0, 1)
ON_GPSIMD_FIRST = (0, 1, 2)

FLOPS = 2 * BATCH * HID * (NG * HID) + 2 * BATCH * HID * (2 * OUT)


def tile_rdecommunicationlstm_pb_t_kernel(
    tc, h1, W_ih1, hh_gates, b_ih1, b_hh1, c_init, mu_W, mu_b, ln_g, ln_b, sig_W, sig_b, out_0, out_1
):
    nc = tc.nc
    with ExitStack() as pools:
        consts = pools.enter_context(tc.tile_pool(name="consts", bufs=1))
        raw_pool = pools.enter_context(tc.tile_pool(name="raw", bufs=5))
        stage = pools.enter_context(tc.tile_pool(name="stage", bufs=2))
        gates = pools.enter_context(tc.tile_pool(name="gates", bufs=2))
        softplus = pools.enter_context(tc.tile_pool(name="softplus", bufs=NBLK))
        psum_t = pools.enter_context(tc.psum_pool(name="psum_t", bufs=2))
        psum_gate = pools.enter_context(tc.psum_pool(name="psum_gate", bufs=4))
        psum_head = pools.enter_context(tc.psum_pool(name="psum_head", bufs=2))
        pools.enter_context(tc.manual_schedule())

        zeros = consts.tile([P, K], BF16)
        nc.vector.memset(zeros[:], 0.0)

        def load_rows(source, pieces=1):
            raw = raw_pool.tile([P, PACK * K], BF16, name="raw")
            width = PACK * K // pieces
            for piece in range(pieces):
                cols = slice(piece * width, (piece + 1) * width)
                nc.sync.dma_start(out=raw[:, cols], in_=source[:, cols])
            return raw

        def h1_rows(n):
            return h1[n * ROWS : (n + 1) * ROWS, :].rearrange("(r j) k -> r (j k)", j=PACK)

        h1_raw = {0: load_rows(h1_rows(0), pieces=2)}
        unit_rows = consts.tile([P, HID], BF16)
        nc.vector.memset(unit_rows[:], 0.0)
        for v, vector in enumerate((hh_gates, b_ih1, b_hh1)):
            nc.sync.dma_start(out=unit_rows[32 * v : 32 * v + NG, :], in_=vector.rearrange("(g k) -> g k", g=NG))
        nc.sync.dma_start(out=unit_rows[96:97, :], in_=c_init.unsqueeze(0))
        w_raw = {}
        for g in GATE_ORDER:
            w_raw[g] = load_rows(
                W_ih1[g * HID : (g + 1) * HID, :].rearrange("(m t) k -> m (t k)", t=PACK),
                pieces=2 if g == GATE_ORDER[0] else 1,
            )
        h1_raw[1] = load_rows(h1_rows(1))
        head_raw = raw_pool.tile([P, PACK * K], BF16, name="raw")
        head_raw_tiles = head_raw[:].rearrange("r (a k) -> r a k", a=PACK)
        nc.sync.dma_start(out=head_raw_tiles[:, 0:2, :], in_=mu_W.rearrange("(a r) k -> r a k", a=2))
        nc.sync.dma_start(out=head_raw_tiles[:, 2:4, :], in_=sig_W.rearrange("(a r) k -> r a k", a=2))
        head_rows = consts.tile([P, 4 * OUT], BF16)
        nc.vector.memset(head_rows[:], 0.0)
        for slot, vector in enumerate((mu_b, sig_b, ln_g, ln_b)):
            nc.sync.dma_start(out=head_rows[0:1, slot * OUT : (slot + 1) * OUT], in_=vector.unsqueeze(0))
        for n in range(2, NBLK):
            h1_raw[n] = load_rows(h1_rows(n))

        warm = consts.tile([P, 1], F32)
        nc.vector.memset(warm[:], 0.0)
        nc.scalar.activation(out=warm[:], in_=warm[:], func=ACT.Sigmoid)
        identity = consts.tile([P, P], F32)
        make_identity(nc, identity[:])
        ones = consts.tile([P, P], BF16)
        nc.vector.memset(ones[:], 1.0)
        minus_half = consts.tile([P, 2, 2], F32)
        nc.vector.memset(minus_half[:], -0.5)
        pick = consts.tile([P, NG + 1], BF16)
        two = consts.tile([P, NG], F32)
        nc.gpsimd.tensor_tensor(out=two[:], in0=identity[:, 0:NG], in1=identity[:, 32 : 32 + NG], op=ALU.add)
        nc.gpsimd.tensor_tensor(out=pick[:, 0:NG], in0=two[:], in1=identity[:, 64 : 64 + NG], op=ALU.add)
        nc.gpsimd.tensor_copy(out=pick[:, NG : NG + 1], in_=identity[:, 96:97])
        per_unit = consts.tile([P, PACK, NG + 1], F32)

        def spread_units():
            units_ps = psum_head.tile([P, PACK, NG + 1], F32, name="head")
            for t in range(PACK):
                nc.tensor.matmul(
                    out=units_ps[:, t, :], lhsT=unit_rows[:].rearrange("v (m t) -> v t m", t=PACK)[:, t, :], rhs=pick[:],
                    start=True, stop=True,
                )
            nc.vector.tensor_copy(out=per_unit[:], in_=units_ps[:])

        def make_diagonals():
            for t in OFF_VECTOR:
                nc.gpsimd.tensor_scalar(
                    out=diag_c[t][:], in0=identity[:], scalar1=per_unit[:, t, NG : NG + 1], scalar2=None, op0=ALU.mult
                )

        diag_c = {}
        for t in OFF_VECTOR:
            diag_c[t] = consts.tile([P, P], F32, name="diag_c%d" % t)

        lin = consts.tile([P, NBLK, 2, PACK, OUT], F32)
        stats = consts.tile([P, NBLK, 2, 2, 3], F32)
        var_eps = consts.tile([P, NBLK, 2, 2], F32)
        var_released = consts.tile([P, NBLK, 2, 2], F32)
        rstd = consts.tile([P, NBLK, 2, 2], F32)

        def grouped_tile():
            return stage.tile([P, ROWS * PACK], BF16, name="grouped", align_bytes=64)

        def transpose_half(raw, half, pool=psum_t, tag="transposed"):
            words = raw[:].bitcast(F32).rearrange("r (a q u) -> r a u q", a=PACK, u=2)
            bank = pool.tile([P, 2, 2, P], F32, tag=tag)
            for a in range(2):
                for u in range(2):
                    nc.tensor.transpose(bank[:, a, u, :], words[:, 2 * half + a, u, :], identity[:])
            return bank

        def copy_half(bank, grouped, half, copy_out):
            grouped_words = grouped[:].bitcast(F32).rearrange("q (a r u) -> q a r u", a=PACK, u=2)
            copy_out(
                out=grouped_words[:, 2 * half : 2 * half + 2, :, :],
                in_=bank[:].rearrange("q a u r -> q a r u"),
            )

        def operand(pool, name):
            codes = pool.tile([P, ROWS], U32, name=name + "_codes", align_bytes=64)
            scales = pool.tile([P, ROWS], U8, name=name + "_scales", align_bytes=64)
            return codes, scales

        def quantise(values, codes_scales, rows=slice(0, ROWS)):
            codes, scales = codes_scales
            nc.vector.quantize_mx(
                out=codes[:, rows].bitcast(FP8X4), scales=scales[:, rows],
                in_=values[:, PACK * rows.start : PACK * rows.stop],
            )

        def prepare_half(raw, grouped, codes_scales, half, copy_out, *bank):
            copy_half(transpose_half(raw, half, *bank), grouped, half, copy_out)
            quantise(grouped, codes_scales, slice(half * ROWS // 2, (half + 1) * ROWS // 2))

        def prepare(raw, copies, pool, name, *bank):
            grouped, codes_scales = grouped_tile(), operand(pool, name)
            for half, copy_out in enumerate(copies):
                prepare_half(raw, grouped, codes_scales, half, copy_out, *bank)
            return codes_scales

        copy_on_vector, copy_on_scalar = nc.vector.tensor_copy, nc.scalar.copy
        h1_banks, h1_grouped, h1_q, w_q = {}, {}, {}, {}
        act, h2, h2_q, sigs, cell_ps, head_ps = {}, {}, {}, {}, {}, {}

        def transpose_h1(n):
            h1_banks[n] = [transpose_half(h1_raw[n], half) for half in range(2)]

        def copy_h1(n, copies):
            h1_grouped[n] = grouped_tile()
            for half, copy_out in enumerate(copies):
                copy_half(h1_banks[n][half], h1_grouped[n], half, copy_out)

        def quantise_h1(n):
            h1_q[n] = operand(stage, "h1")
            quantise(h1_grouped[n], h1_q[n])

        def gate(n, g, tiles=range(PACK)):
            (codes, scales), (w_codes, w_scales) = h1_q[n], w_q[g]
            if (n, g) not in act:
                act[n, g] = gates.tile([P, PACK, ROWS], F32, name="gate%d" % g)
            for t in tiles:
                units = slice(t * P, (t + 1) * P)
                gate_ps = psum_gate.tile([P, ROWS], F32, tag="gate")
                nc.tensor.matmul_mx(
                    out=gate_ps[:],
                    lhsT=w_codes[:, units].bitcast(FP8X4), lhsT_scale=w_scales[:, units],
                    rhs=codes[:].bitcast(FP8X4), rhs_scale=scales[:],
                    start=True, stop=True,
                )
                nc.scalar.activation(
                    out=act[n, g][:, t, :], in_=gate_ps[:],
                    func=ACT.Tanh if g == GATE_G else ACT.Sigmoid,
                    bias=per_unit[:, t, g : g + 1], scale=1.0,
                )

        def input_times_candidate(engine, n, tiles):
            engine.tensor_tensor(
                out=act[n, GATE_I][:, tiles, :], in0=act[n, GATE_I][:, tiles, :], in1=act[n, GATE_G][:, tiles, :],
                op=ALU.mult,
            )

        def open_cell(n, t):
            cell_ps[n, t] = psum_head.tile([P, ROWS], F32, name="head")
            nc.tensor.matmul(
                out=cell_ps[n, t][:], lhsT=diag_c[t][:], rhs=act[n, GATE_F][:, t, :], start=True, stop=False
            )

        def close_cell(n, t):
            nc.tensor.matmul(
                out=cell_ps[n, t][:], lhsT=identity[:], rhs=act[n, GATE_I][:, t, :], start=False, stop=True
            )

        def new_cell(n, t):
            nc.vector.scalar_tensor_tensor(
                out=act[n, GATE_F][:, t, :], in0=act[n, GATE_F][:, t, :], scalar=per_unit[:, t, NG : NG + 1],
                in1=act[n, GATE_I][:, t, :], op0=ALU.mult, op1=ALU.add,
            )

        def tanh_cell(n, t, cell):
            nc.scalar.activation(out=act[n, GATE_F][:, t, :], in_=cell, func=ACT.Tanh)

        def hidden(n):
            h2[n] = stage.tile([P, ROWS * PACK], BF16, name="h2", align_bytes=64)
            nc.vector.tensor_tensor(
                out=h2[n][:].rearrange("m (c i t) -> m c t i", i=4, t=PACK),
                in0=act[n, GATE_O][:].rearrange("m t (c i) -> m c t i", i=4),
                in1=act[n, GATE_F][:].rearrange("m t (c i) -> m c t i", i=4),
                op=ALU.mult,
            )

        def quantise_hidden(n):
            h2_q[n] = operand(stage, "h2")
            quantise(h2[n], h2_q[n])

        def head_product(n, j):
            codes, scales = h2_q[n]
            rows = slice(j * P, (j + 1) * P)
            head_ps[n, j] = psum_head.tile([P, 2 * OUT], F32, name="head")
            nc.tensor.matmul_mx(
                out=head_ps[n, j][:],
                lhsT=codes[:, rows].bitcast(FP8X4), lhsT_scale=scales[:, rows],
                rhs=head_q[0][:].bitcast(FP8X4), rhs_scale=head_q[1][:],
                start=True, stop=True,
            )

        def head_sum(n, j):
            nc.vector.tensor_tensor(
                out=lin[:, n, :, j, :], in0=head_ps[n, j][:].rearrange("r (h c) -> r h c", h=2), in1=head_bias,
                op=ALU.add,
            )

        def row_stats(n, pairs=(0, 1)):
            for h in pairs:
                nc.vector.bn_stats(
                    out=stats[:, n, h, :, :].rearrange("r e s -> r (e s)"),
                    in_=lin[:, n, 0, 2 * h : 2 * h + 2, :].rearrange("r e c -> r c e"),
                )

        def row_var(n, pairs=slice(0, 2)):
            nc.vector.tensor_scalar(
                out=var_eps[:, n, pairs, :], in0=stats[:, n, pairs, :, 2],
                scalar1=1.0 / OUT, scalar2=LN_EPS, op0=ALU.mult, op1=ALU.add,
            )
            nc.gpsimd.tensor_copy(out=var_released[:, n, pairs, :], in_=var_eps[:, n, pairs, :])

        def row_rstd(n, pairs=slice(0, 2)):
            nc.gpsimd.tensor_tensor(
                out=rstd[:, n, pairs, :], in0=var_released[:, n, pairs, :], in1=minus_half[:, pairs, :], op=ALU.pow
            )

        def sigmoid_spread(n, tiles=slice(0, PACK)):
            if n not in sigs:
                sigs[n] = softplus.tile([P, PACK, OUT], F32, name="sigs")
            nc.scalar.activation(
                out=sigs[n][:, tiles, :], in_=lin[:, n, 1, tiles, :], func=ACT.Sigmoid, bias=0.0, scale=-1.0
            )

        def centre(n, tiles=range(PACK)):
            for j in tiles:
                nc.vector.scalar_tensor_tensor(
                    out=lin[:, n, 0, j, :], in0=lin[:, n, 0, j, :], scalar=stats[:, n, j // 2, j % 2, 1:2],
                    in1=ln_g_all, op0=ALU.subtract, op1=ALU.mult,
                )

        def scale(n, tiles=range(PACK)):
            for j in tiles:
                nc.vector.scalar_tensor_tensor(
                    out=lin[:, n, 0, j, :], in0=lin[:, n, 0, j, :], scalar=rstd[:, n, j // 2, j % 2 : j % 2 + 1], in1=ln_b_all,
                    op0=ALU.mult, op1=ALU.add,
                )

        def store_mu(n):
            nc.sync.dma_start(
                out=out_0[n * ROWS : (n + 1) * ROWS, :].rearrange("(r j) c -> r j c", j=PACK),
                in_=lin[:, n, 0, :, :],
            )

        def softplus_log(n, tiles=slice(0, PACK)):
            v, sig = lin[:, n, 1, tiles, :], sigs[n][:, tiles, :]
            nc.scalar.activation(out=sig, in_=sig, func=ACT.Ln, bias=SIG_SCALE * SIG_FLOOR, scale=SIG_SCALE)
            nc.vector.scalar_tensor_tensor(out=v, in0=sig, scalar=-1.0, in1=v, op0=ALU.mult, op1=ALU.max)
            nc.sync.dma_start(
                out=out_1[n * ROWS : (n + 1) * ROWS, :].rearrange("(r j) c -> r j c", j=PACK)[:, tiles, :], in_=v
            )

        def keep_tensor_busy(products):
            for product in range(products):
                idle_ps = psum_gate.tile([P, ROWS], F32, tag="gate")
                nc.tensor.matmul(out=idle_ps[:], lhsT=zeros[:, 0:P], rhs=zeros[:], start=True, stop=True)

        keep_tensor_busy(3)
        h1_q[0] = prepare(h1_raw[0], (copy_on_vector, copy_on_scalar), stage, "h1")
        keep_tensor_busy(1)
        spread_units()
        w_q[GATE_I] = prepare(
            w_raw[GATE_I], (copy_on_scalar, copy_on_scalar), consts, "w%d" % GATE_I, psum_gate, "gate"
        )
        make_diagonals()

        def prepare_gate(g):
            w_q[g] = prepare(w_raw[g], (copy_on_vector, copy_on_vector), consts, "w%d" % g)

        g_grouped, w_q[GATE_G] = grouped_tile(), operand(consts, "w%d" % GATE_G)
        prepare_half(w_raw[GATE_G], g_grouped, w_q[GATE_G], 0, copy_on_vector)
        gate(0, GATE_I, (0, 1))
        prepare_half(w_raw[GATE_G], g_grouped, w_q[GATE_G], 1, copy_on_vector)
        gate(0, GATE_I, (2, 3))

        def cell(n, on_tensor, between=None):
            on_vector = [t for t in reversed(range(PACK)) if t not in on_tensor]
            for t in on_vector:
                new_cell(n, t)
            for t in on_tensor:
                open_cell(n, t)
            if between:
                between()
            for t in on_tensor:
                close_cell(n, t)
            for t in on_vector:
                tanh_cell(n, t, act[n, GATE_F][:, t, :])
            for t in on_tensor:
                tanh_cell(n, t, cell_ps[n, t][:])

        spread = consts.tile([P, 4 * OUT], F32)
        head_bias = spread[:, 0 : 2 * OUT].rearrange("r (h c) -> r h c", h=2)
        ln_g_all = spread[:, 2 * OUT : 3 * OUT]
        ln_b_all = spread[:, 3 * OUT : 4 * OUT]

        def repeat_heads(half):
            bank = psum_head.tile([P, 2 * OUT], F32, name="head")
            cols = slice(half * 2 * OUT, (half + 1) * 2 * OUT)
            nc.tensor.matmul(out=bank[:], lhsT=ones[:], rhs=head_rows[:, cols], start=True, stop=True)
            return bank

        def spread_heads(half, bank):
            nc.vector.tensor_copy(out=spread[:, half * 2 * OUT : (half + 1) * 2 * OUT], in_=bank[:])

        prepare_gate(GATE_F)
        gate(0, GATE_G)
        prepare_gate(GATE_O)
        gate(0, GATE_F)
        transpose_h1(1)
        for t in ON_GPSIMD_FIRST:
            input_times_candidate(nc.gpsimd, 0, slice(t, t + 1))
        gate(0, GATE_O)
        input_times_candidate(nc.vector, 0, slice(len(ON_GPSIMD_FIRST), PACK))
        copy_h1(1, (copy_on_vector, copy_on_vector))
        head_banks = []
        cell(0, OFF_VECTOR[:1], lambda: head_banks.extend([transpose_half(head_raw, half) for half in range(2)]))
        quantise_h1(1)
        head_grouped, head_q = grouped_tile(), operand(consts, "head")
        for half in range(2):
            copy_half(head_banks[half], head_grouped, half, copy_on_vector)
        quantise(head_grouped, head_q)
        spread_heads(0, repeat_heads(0))

        spread_done = 0
        for n in range(1, NBLK):
            last = n - 1
            gate(n, GATE_I)
            if n < NBLK - 2:
                transpose_h1(n + 1 if n == 1 else n + 2)
            hidden(last)
            if n > 2:
                scale(n - 3, (3,))
                store_mu(n - 3)
            quantise_hidden(last)
            if n == 1:
                copy_h1(2, (copy_on_vector, copy_on_vector))
            elif n < NBLK - 1:
                quantise_h1(n + 1)
            else:
                centre(n - 2, (0, 1))
            gate(n, GATE_G)
            gate(n, GATE_F, (0,))
            head_product(last, 0)
            head_product(last, 1)
            if n > 1:
                row_var(n - 2)
            gate(n, GATE_F, (1, 2))
            head_sum(last, 0)
            head_product(last, 2)
            gate(n, GATE_F, (3,))
            head_sum(last, 1)
            head_product(last, 3)
            head_sum(last, 2)
            head_sum(last, 3)
            row_stats(last)
            on_gpsimd = ON_GPSIMD_FIRST if n == 1 else OFF_VECTOR
            for t in on_gpsimd:
                input_times_candidate(nc.gpsimd, n, slice(t, t + 1))
            if n > 1:
                row_rstd(n - 2)
            gate(n, GATE_O)
            if n == 1:
                transpose_h1(3)
            if n < NBLK - 2:
                copy_h1(n + 2, (copy_on_scalar, copy_on_scalar))
            input_times_candidate(nc.vector, n, slice(len(on_gpsimd), PACK))
            if n > 1:
                centre(n - 2, (2,))
            if n >= NBLK - 2:
                sigmoid_spread(spread_done)
                spread_done += 1
            if n == 1:
                cell(n, OFF_VECTOR[:1])
                quantise_h1(2)
                spread_heads(1, repeat_heads(1))
            else:
                cell(n, OFF_VECTOR)
                centre(n - 2, (0, 1, 3) if n < NBLK - 1 else (3,))
                scale(n - 2, (0, 1, 2))

        last = NBLK - 1
        centre(last - 1, (0, 1))
        hidden(last)
        scale(last - 2, (3,))
        store_mu(last - 2)
        quantise_hidden(last)
        centre(last - 1, (2, 3))
        row_var(last - 1)
        row_rstd(last - 1)
        for n in range(spread_done, last):
            sigmoid_spread(n)
        for j in range(PACK):
            head_product(last, j)
            head_sum(last, j)
            sigmoid_spread(last, slice(j, j + 1))
            if j % 2 == 1:
                pair = slice(j // 2, j // 2 + 1)
                row_stats(last, (j // 2,))
                row_var(last, pair)
                row_rstd(last, pair)
        scale(last - 1)
        store_mu(last - 1)
        centre(last)
        softplus_log(0)
        scale(last)
        store_mu(last)
        for n in range(1, last):
            softplus_log(n)
        for half in range(2):
            softplus_log(last, slice(2 * half, 2 * half + 2))
